import numpy as np
import ml_dtypes


def mxq(x, axis, fmt="e4m3"):
    dtype, down = {"e4m3": (ml_dtypes.float8_e4m3fn, 7), "e5m2": (ml_dtypes.float8_e5m2, 14)}[fmt]
    v = np.moveaxis(np.asarray(x, np.float32).astype(ml_dtypes.bfloat16).astype(np.float64), axis, -1)
    blocks = v.reshape(v.shape[:-1] + (-1, 32))
    amax = np.abs(blocks).max(-1, keepdims=True)
    byte = np.maximum(np.where(amax > 0, np.frexp(amax)[1] - 1 + 127, 0) - down, 1)
    scale = np.exp2(byte - 127.0)
    codes = (blocks / scale).astype(np.float32).astype(dtype).astype(np.float64)
    return np.moveaxis((codes * scale).reshape(v.shape), -1, axis)


WIDE = False


def mx_kscale(k):
    if not WIDE:
        return np.ones(k)
    levels = np.array([10, -10, 5, -5, 0])
    if k % 512:
        return np.exp2(np.random.permutation(np.resize(levels, k // 32))).repeat(32)
    a = np.empty((k // 512, 16))
    for p in range(k // 512):
        a[p, :8] = np.random.permutation(np.resize(levels, 8))
        for g in range(8):
            far = levels[np.abs(levels - a[p, g]) >= 10]
            a[p, g + 8] = far[np.random.randint(len(far))]
    return np.exp2(a.ravel()).repeat(32)


BF16 = ml_dtypes.bfloat16


def bf(x):
    return np.asarray(x, np.float32).astype(BF16)


def f64(x):
    return np.asarray(x).astype(np.float64)


E2M1 = np.array([0.0, 0.5, 1.0, 1.5, 2.0, 3.0, 4.0, 6.0, -0.0, -0.5, -1.0, -1.5, -2.0, -3.0, -4.0, -6.0])


def pack_weight(w, fmt):
    k, n = w.shape
    w = f64(bf(w)).reshape(k // 32, 32, n)
    amax = np.abs(w).max(1)
    if fmt == "e4m3":
        byte = np.frexp(amax)[1] - 1 + 127 - 7
    else:
        mant, ex = np.frexp(amax / 6.0)
        byte = np.where(mant > 0.5, ex, ex - 1) + 127
    byte = np.clip(np.where(amax > 0, byte, 1), 1, 254)
    scaled = (w * np.exp2(127.0 - byte)[:, None, :]).reshape(k, n).astype(np.float32)
    by_word = np.ascontiguousarray(scaled.reshape(k // 512, 128, 4, n).transpose(0, 1, 3, 2))
    if fmt == "e4m3":
        words = by_word.astype(ml_dtypes.float8_e4m3fn).view(np.uint8)
    else:
        c = by_word.astype(ml_dtypes.float4_e2m1fn).view(np.uint8) & 0xF
        words = c[..., 0::2] | (c[..., 1::2] << 4)
    return np.ascontiguousarray(words), np.ascontiguousarray(byte.astype(np.uint8).reshape(k // 512, 16, n))


def unpack_weight(words, scales, fmt):
    g, p, n, _ = words.shape
    if fmt == "e4m3":
        vals = np.ascontiguousarray(words).view(ml_dtypes.float8_e4m3fn).astype(np.float64)
    else:
        nib = np.empty((g, p, n, 4), np.uint8)
        nib[..., 0::2] = words & 0xF
        nib[..., 1::2] = words >> 4
        vals = E2M1[nib]
    vals = vals * np.repeat(np.exp2(scales.astype(np.float64) - 127.0), 8, axis=1)[..., None]
    return vals.transpose(0, 1, 3, 2).reshape(g * 512, n)
def pack4(w):
    words, scales = pack_weight(w, "e2m1")
    return words.reshape(words.shape[0], 128, -1), scales


def unpack4(words, scales):
    return unpack_weight(words.reshape(words.shape[0], 128, -1, 2), scales, "e2m1")


B, HALF, MID = 512, 512, 2048
D = 2 * HALF


def draw0():
    s, t = mx_kscale(MID), mx_kscale(MID)
    x = bf(np.random.standard_normal((B, D)))
    h3 = bf(np.maximum(np.random.standard_normal((B, MID)), 0.0) * s)
    W4_words, W4_scales = pack4(np.random.standard_normal((MID, MID)) * np.sqrt(2.0 / MID) / s[:, None] * t)
    b4 = bf(np.random.standard_normal(MID) * 0.2 * t)
    W5_words, W5_scales = pack4(np.random.standard_normal((MID, HALF)) * np.sqrt(2.0 / MID) / t[:, None])
    b5 = bf(np.random.standard_normal(HALF) * 0.2)
    return {"x": x,
            "h3": h3,
            "W4_words": W4_words,
            "W4_scales": W4_scales,
            "b4": b4,
            "W5_words": W5_words,
            "W5_scales": W5_scales,
            "b5": b5}


def core(x, h3, W4_words, W4_scales, b4, W5_words, W5_scales, b5):
    x = f64(x)
    even = x[:, 0::2]
    odd = x[:, 1::2]
    h4 = np.maximum((mxq(f64(h3), 1, "e4m3") @ unpack4(W4_words, W4_scales)) + f64(b4), 0.0)
    m = (mxq(h4, 1, "e4m3") @ unpack4(W5_words, W5_scales)) + f64(b5)
    transformed = even + m
    return np.stack([transformed, odd], axis=2).reshape(B, -1)


def e4m3fn_bytes(y):
    return np.clip(np.asarray(y, np.float64), -448.0, 448.0).astype(np.float32).astype(ml_dtypes.float8_e4m3fn).view(np.uint8)


def e4m3fn_values(b):
    return np.asarray(b, np.uint8).view(ml_dtypes.float8_e4m3fn).astype(np.float64)


def setup_inputs():
    d = draw0()
    x0 = np.asarray(d['h3']).astype(np.float64)
    s = (np.max(np.abs(x0), axis=(0,), keepdims=True) / 448.0).astype(np.float32)
    out = {}
    for k, v in d.items():
        if k == 'h3':
            out['h3_bytes'] = e4m3fn_bytes(x0 / s.astype(np.float64))
            out['h3_scale'] = s
        else:
            out[k] = v
    return out


def reference(x, h3_bytes, h3_scale, W4_words, W4_scales, b4, W5_words, W5_scales, b5):
    return core(x, e4m3fn_values(h3_bytes) * h3_scale.astype(np.float64), W4_words, W4_scales, b4, W5_words, W5_scales, b5)

@@ -1,0 +1,392 @@
+from contextlib import ExitStack
+
+import concourse.mybir as mybir
+from concourse.masks import make_identity
+
+B, HALF, MID = 512, 512, 2048
+FLOPS = 2 * B * MID * MID + 2 * B * MID * HALF
+
+P = 128
+TT = B // P
+NG = MID // 512
+F32 = mybir.dt.float32
+BF16 = mybir.dt.bfloat16
+U8 = mybir.dt.uint8
+U32 = mybir.dt.uint32
+I32 = mybir.dt.int32
+FP8 = mybir.dt.float8_e4m3fn
+FP8X4 = mybir.dt.float8_e4m3fn_x4
+FP4X4 = mybir.dt.float4_e2m1fn_x4
+ALU = mybir.AluOpType
+ACT = mybir.ActivationFunctionType
+
+NM = 3
+TILES = [(g, j) for g in range(NM) for j in range(4)]
+SWEEP = 6
+EXIT_V = (1, 3, 5, 7, 9)
+
+
+def tile_additivecoupling_pa_w4_kernel(
+    tc, x, h3_bytes, h3_scale, W4_words, W4_scales, b4, W5_words, W5_scales, b5, out
+):
+    nc = tc.nc
+    with ExitStack() as ctx:
+        keep = ctx.enter_context(tc.tile_pool(name="keep", bufs=1))
+        work = ctx.enter_context(tc.tile_pool(name="work", bufs=2))
+        psum = ctx.enter_context(tc.psum_pool(name="psum", bufs=1))
+        ctx.enter_context(tc.manual_schedule())
+
+        ident = keep.tile([P, P], F32, name="ident")
+        make_identity(nc, ident[:])
+        w4s = keep.tile([P, NG, MID], U8, name="w4s", align_bytes=64)
+        w5s = keep.tile([P, NG, HALF], U8, name="w5s", align_bytes=64)
+        warm = keep.tile([P, 1], F32, name="warm")
+        nc.vector.memset(warm[:], 0.0)
+        srows = keep.tile([P, P], F32, name="srows")
+        nc.vector.memset(srows[:], 0.0)
+        brows = keep.tile([P, P], BF16, name="brows")
+        nc.vector.memset(brows[:], 0.0)
+        nc.vector.memset(w4s[:].rearrange("p g n -> p (g n)").bitcast(I32), 0)
+        nc.gpsimd.memset(w5s[:].rearrange("p g n -> p (g n)").bitcast(I32), 0)
+        warm2 = keep.tile([P, 1], F32, name="warm2")
+        nc.scalar.activation(out=warm2[:], in_=warm[:], func=ACT.Relu)
+
+        h3v = h3_bytes.rearrange("(p i) k -> p i k", i=TT)
+        hb0 = keep.tile([P, TT, 512], U8, name="hb0", align_bytes=64)
+        hb1 = keep.tile([P, TT, 512], U8, name="hb1", align_bytes=64)
+        hb23 = keep.tile([P, TT, 1024], U8, name="hb23", align_bytes=64)
+        hb = [hb0, hb1, hb23[:, :, 0:512], hb23[:, :, 512:1024]]
+        sc, w4a = [], []
+        w4b = keep.tile([P, NG, 1024], U8, name="w4b", align_bytes=64)
+        w5 = keep.tile([P, NG, 1024], U8, name="w5", align_bytes=64)
+        for g in range(NG):
+            s_g = keep.tile([P, 512], F32, name=f"sc{g}", align_bytes=64)
+            sc.append(s_g)
+        w4a0 = keep.tile([P, 1024 * NM], U8, name="w4a0", align_bytes=64)
+        w4a1 = keep.tile([P, 1024 * NM], U8, name="w4a1", align_bytes=64)
+        w4a23 = keep.tile([P, 2, 1024 * NM], U8, name="w4a23", align_bytes=64)
+        w4a = [w4a0, w4a1, w4a23[:, 0, :], w4a23[:, 1, :]]
+        b4bc = keep.tile([P, 512], BF16, name="b4bc")
+        b5bc = keep.tile([P, HALF], BF16, name="b5bc")
+
+        def load_w4(g):
+            nc.sync.dma_start(out=w4a[g][:].bitcast(I32), in_=W4_words[g, :, 0 : 1024 * NM].bitcast(I32))
+
+        def load_scales(dst, src):
+            for r in range(4):
+                nc.sync.dma_start(
+                    out=dst[r:P:32, :, :].bitcast(I32), in_=src[:, r:16:4, :].rearrange("g q n -> q g n").bitcast(I32)
+                )
+
+        s0tile = keep.tile([P, 4], F32, name="s0tile")
+        with nc.allow_non_contiguous_dma(reason="512 scales, one to a partition and column"):
+            nc.sync.dma_start(out=s0tile[:], in_=h3_scale[:, 0:512].rearrange("o (m p) -> p (o m)", p=P))
+        nc.sync.dma_start(out=hb0[:], in_=h3v[:, :, 0:512])
+        nc.sync.dma_start(out=srows[0:16, :], in_=h3_scale.rearrange("o (c p) -> (o c) p", p=P))
+        nc.sync.dma_start(out=hb1[:], in_=h3v[:, :, 512:1024])
+        load_scales(w4s, W4_scales)
+        nc.sync.dma_start(out=hb23[:], in_=h3v[:, :, 1024:2048])
+        load_w4(0)
+        nc.sync.dma_start(out=brows[0:12, :], in_=b4[0 : 512 * NM].rearrange("(c p) -> c p", p=P))
+        load_w4(1)
+        nc.sync.dma_start(
+            out=w4a23[:].bitcast(I32), in_=W4_words[2:4, :, 0 : 1024 * NM].rearrange("g p n -> p g n").bitcast(I32)
+        )
+        nc.sync.dma_start(out=w4b[:].bitcast(I32), in_=W4_words[:, :, 1024 * NM :].rearrange("g p n -> p g n").bitcast(I32))
+        load_scales(w5s, W5_scales)
+        nc.sync.dma_start(out=w5[:].bitcast(I32), in_=W5_words.rearrange("g p n -> p g n").bitcast(I32))
+        xt = keep.tile([P, TT, 2 * HALF], BF16, name="xt")
+        nc.sync.dma_start(out=b5bc[:], in_=b5.partition_broadcast(P))
+        nc.sync.dma_start(out=xt[:], in_=x.rearrange("(p i) c -> p i c", i=TT))
+        nc.sync.dma_start(out=b4bc[:], in_=b4[512 * NM :].partition_broadcast(P))
+
+        h3g, h3q, h3s, prods = [], [], [], {}
+        for g in range(NG):
+            t_g = work.tile([P, B, 4], BF16, name="h3g", tag="h3g", bufs=2, align_bytes=64)
+            q_g = keep.tile([P, B], U32, name=f"h3q{g}", align_bytes=64)
+            s_g = keep.tile([P, B], U8, name=f"h3s{g}", align_bytes=64)
+            h3g.append(t_g)
+            h3q.append(q_g)
+            h3s.append(s_g)
+
+        def product(g, i):
+            t = work.tile([P, 512], BF16, name="prod", tag="prod", bufs=6, align_bytes=64)
+            nc.vector.tensor_tensor(out=t[:], in0=hb[g][:, i, :].bitcast(FP8), in1=sc[g][:], op=ALU.mult)
+            prods[g, i] = t
+
+        def transpose_pair(g, half):
+            bank = psum.tile([P, 2, 2, P], F32, name="tr", tag="tr", bufs=2)
+            for ii in range(2):
+                words = prods[g, 2 * half + ii][:].bitcast(F32)
+                for u in range(2):
+                    nc.tensor.transpose(bank[:, ii, u, :], words[:, u::2], ident[:])
+            dst = h3g[g][:, 256 * half : 256 * (half + 1), :].rearrange("p c t -> p (c t)").bitcast(F32)
+            nc.scalar.copy(
+                out=dst.rearrange("p (i m u) -> p i m u", i=2, u=2), in_=bank[:].rearrange("p i u m -> p i m u")
+            )
+
+        def quantise_h3(g):
+            cols = slice(0, B)
+            nc.vector.quantize_mx(
+                out=h3q[g][:, cols].bitcast(FP8X4),
+                scales=h3s[g][:, cols],
+                in_=h3g[g][:, cols, :].rearrange("p c t -> p (c t)"),
+            )
+
+        acc = {}
+
+        def pass1(n, g):
+            if g == 0:
+                bank = psum.tile([P, B], F32, name="acc", tag=f"b{n % 6}", bufs=1)
+                acc[n] = bank
+            c = 4 * TILES[n][0] + TILES[n][1]
+            w = w4a[g][:, 256 * c : 256 * (c + 1)]
+            nc.tensor.matmul_mx(
+                out=acc[n][:],
+                lhsT=w.bitcast(FP4X4),
+                lhsT_scale=w4s[:, g, P * c : P * (c + 1)],
+                rhs=h3q[g][:].bitcast(FP8X4),
+                rhs_scale=h3s[g][:],
+                start=(g == 0),
+                stop=(g == NG - 1),
+            )
+
+        h4n = []
+        for g in range(NM):
+            t_g = keep.tile([P, 4, B], BF16, name=f"h4n{g}", align_bytes=64)
+            h4n.append(t_g)
+
+        def exit1(n):
+            g, j = TILES[n]
+            c = 4 * g + j
+            h4 = work.tile([P, B], BF16, name="h4", tag="h4", bufs=12, align_bytes=64)
+            if n in EXIT_V:
+                nc.vector.tensor_scalar(
+                    out=h4[:], in0=acc[n][:], scalar1=bt[:, c : c + 1], scalar2=0.0, op0=ALU.add, op1=ALU.max
+                )
+            else:
+                nc.scalar.activation(out=h4[:], in_=acc[n][:], func=ACT.Relu, bias=bt[:, c : c + 1])
+            nc.sync.dma_start(out=h4n[g][32 * j : 32 * (j + 1), :, :].rearrange("a s c -> a (s c)"), in_=h4[:])
+
+        h4q, h4s = [], []
+        for g in range(NG):
+            q_g = keep.tile([P, B], U32, name=f"h4q{g}", align_bytes=64)
+            s_g = keep.tile([P, B], U8, name=f"h4s{g}", align_bytes=64)
+            h4q.append(q_g)
+            h4s.append(s_g)
+
+        inter = {}
+
+        def interleave(g, copy, lo, hi):
+            if g not in inter:
+                t = work.tile([P, B, 4], BF16, name="h4i", tag="h4i", bufs=3, align_bytes=64)
+                inter[g] = t
+            copy(out=inter[g][:, lo:hi, :], in_=h4n[g][:, :, lo:hi].rearrange("p t c -> p c t"))
+
+        def quantise_h4(g, lo=0, hi=B):
+            nc.vector.quantize_mx(
+                out=h4q[g][:, lo:hi].bitcast(FP8X4),
+                scales=h4s[g][:, lo:hi],
+                in_=inter[g][:, lo:hi, :].rearrange("p c t -> p (c t)"),
+            )
+
+        h4t = {}
+
+        def group_tokens(i):
+            o = 3
+            bank = psum.tile([P, 512], F32, name="acc", tag=f"b{i % 2}", bufs=1)
+            cols = slice(P * i, P * (i + 1))
+            for g in range(NG):
+                nc.tensor.matmul_mx(
+                    out=bank[:],
+                    lhsT=h3q[g][:, cols].bitcast(FP8X4),
+                    lhsT_scale=h3s[g][:, cols],
+                    rhs=w4b[:, g, 1024 * (o - NM) : 1024 * (o - NM + 1)].bitcast(FP4X4),
+                    rhs_scale=w4s[:, g, 512 * o : 512 * (o + 1)],
+                    start=(g == 0),
+                    stop=(g == NG - 1),
+                )
+            return bank
+
+        def add_b4(i, bank):
+            t = work.tile([P, 512], BF16, name="h4t", tag="h4t", bufs=4, align_bytes=64)
+            order = "q (p u e) -> q u p e"
+            nc.vector.tensor_tensor(
+                out=t[:].rearrange("q (u p e) -> q u p e", u=2, e=2),
+                in0=bank[:].rearrange(order, u=2, e=2),
+                in1=b4bc[:].rearrange(order, u=2, e=2),
+                op=ALU.add,
+            )
+            h4t[i] = t
+
+        turned = {}
+
+        def turn_tokens(i):
+            bank = psum.tile([P, 2, P], F32, name="tr", tag="tr", bufs=2)
+            words = h4t[i][:].bitcast(F32)
+            for u in range(2):
+                nc.tensor.transpose(bank[:, u, :], words[:, P * u : P * (u + 1)], ident[:])
+            r = work.tile([P, P, 4], BF16, name="h4r", tag="h4r", bufs=4, align_bytes=64)
+            nc.scalar.activation(
+                out=r[:].rearrange("p m (u e) -> p m u e", u=2),
+                in_=bank[:].rearrange("p u m -> p (u m)").bitcast(BF16).rearrange("p (u m e) -> p m u e", u=2, e=2),
+                func=ACT.Relu,
+            )
+            turned[i] = r
+
+        def quantise_turned(i):
+            cols = slice(P * i, P * (i + 1))
+            nc.vector.quantize_mx(
+                out=h4q[3][:, cols].bitcast(FP8X4),
+                scales=h4s[3][:, cols],
+                in_=turned[i][:].rearrange("p m t -> p (m t)"),
+            )
+
+        acc2 = {}
+
+        def pass2(i, g):
+            if g == 0:
+                bank = psum.tile([P, HALF], F32, name="acc", tag=f"b{2 + i}", bufs=1)
+                acc2[i] = bank
+            cols = slice(P * i, P * (i + 1))
+            nc.tensor.matmul_mx(
+                out=acc2[i][:],
+                lhsT=h4q[g][:, cols].bitcast(FP8X4),
+                lhsT_scale=h4s[g][:, cols],
+                rhs=w5[:, g, :].bitcast(FP4X4),
+                rhs_scale=w5s[:, g, :],
+                start=(g == 0),
+                stop=(g == NG - 1),
+            )
+
+        outv = out.rearrange("(p i) c -> p i c", i=TT)
+
+        outt = []
+        for i in range(TT):
+            o_i = keep.tile([P, HALF, 2], F32, name=f"o{i}")
+            outt.append(o_i)
+
+        def finish_add(i):
+            nc.vector.tensor_tensor(out=pair[:, i, 0, :], in0=acc2[i][:], in1=pair[:, i, 0, :], op=ALU.add)
+
+        def out_pairs(i, copy, lo, hi):
+            copy(out=outt[i][:, lo:hi, :], in_=pair[:, i, :, lo:hi].rearrange("p r j -> p j r"))
+            start = 0 if i < 3 else lo
+            if hi == HALF or i == 3:
+                nc.sync.dma_start(
+                    out=outv[:, i, 2 * start : 2 * hi], in_=outt[i][:, start:hi, :].rearrange("p j r -> p (j r)")
+                )
+
+        def spread(bank, cols, first):
+            for m in range(4):
+                nc.tensor.transpose(bank[:, m, :], cols[:, first + m : first + m + 1].to_broadcast([P, P]), ident[:])
+
+        def scale_bank(g):
+            bank = psum.tile([P, 4, P], F32, name="acc", tag=f"b{g}", bufs=1)
+            if g == 0:
+                spread(bank, s0tile, 0)
+            else:
+                spread(bank, stile, 4 * g)
+            return bank
+
+        def scale_copy(g, bank, copy):
+            copy(out=sc[g][:], in_=bank[:].rearrange("p m n -> p (m n)"))
+
+        scale_copy(0, scale_bank(0), nc.vector.tensor_copy)
+        stile = keep.tile([P, 16], F32, name="stile")
+        sbank = psum.tile([P, P], F32, name="tr", tag="tr", bufs=2)
+        nc.tensor.transpose(sbank[:], srows[:], ident[:])
+        nc.scalar.copy(out=stile[:], in_=sbank[:, 0:16])
+        scale_copy(1, scale_bank(1), nc.scalar.copy)
+        bt = keep.tile([P, 12], F32, name="bt")
+
+        pair = keep.tile([P, TT, 2, HALF], F32, name="pair")
+
+        def x_pairs(i):
+            nc.scalar.activation(out=pair[:, i, 1, :], in_=xt[:, i, 1::2], func=ACT.Copy)
+            nc.vector.tensor_tensor(out=pair[:, i, 0, :], in0=xt[:, i, 0::2], in1=b5bc[:], op=ALU.add)
+
+        def turn_b4():
+            browsf = keep.tile([P, P], F32, name="browsf")
+            nc.gpsimd.tensor_copy(out=browsf[:], in_=brows[:])
+            bbank = psum.tile([P, P], F32, name="tr", tag="tr", bufs=2)
+            nc.tensor.transpose(bbank[:], browsf[:], ident[:])
+            nc.scalar.copy(out=bt[:], in_=bbank[:, 0:12])
+
+        for g in range(NG):
+            if g == 2:
+                turn_b4()
+            product(g, 0)
+            product(g, 1)
+            transpose_pair(g, 0)
+            product(g, 2)
+            product(g, 3)
+            if g > 0:
+                quantise_h3(g - 1)
+            transpose_pair(g, 1)
+            if g == 0:
+                for later in range(2, NG):
+                    scale_copy(later, scale_bank(later), nc.scalar.copy)
+            if g > 0:
+                for n in range(SWEEP):
+                    pass1(n, g - 1)
+        quantise_h3(NG - 1)
+        for n in range(SWEEP):
+            pass1(n, NG - 1)
+            exit1(n)
+        V, S = nc.vector.tensor_copy, nc.scalar.copy
+
+        for n in range(SWEEP, len(TILES)):
+            for g in range(NG):
+                pass1(n, g)
+            exit1(n)
+            if n < SWEEP + TT:
+                x_pairs(n - SWEEP)
+            if n == 9:
+                interleave(0, V, 0, 256)
+                interleave(0, S, 256, B)
+        quantise_h4(0)
+        add_b4(0, group_tokens(0))
+        interleave(1, V, 0, 256)
+        interleave(1, S, 256, B)
+        add_b4(1, group_tokens(1))
+        quantise_h4(1)
+        add_b4(2, group_tokens(2))
+        turn_tokens(0)
+        turn_tokens(1)
+        b3 = group_tokens(3)
+        add_b4(3, b3)
+        interleave(2, V, 0, 256)
+        interleave(2, S, 256, 512)
+        for i in range(2):
+            pass2(i, 0)
+            pass2(i, 1)
+        turn_tokens(2)
+        turn_tokens(3)
+        quantise_h4(2, 0, 256)
+        quantise_turned(0)
+        quantise_turned(1)
+        quantise_h4(2, 256, 512)
+        for i in range(2):
+            pass2(i, 2)
+            pass2(i, 3)
+        for i in range(2, 4):
+            pass2(i, 0)
+            pass2(i, 1)
+        quantise_turned(2)
+        finish_add(0)
+        quantise_turned(3)
+        out_pairs(0, S, 0, 256)
+        out_pairs(0, V, 256, HALF)
+        finish_add(1)
+        out_pairs(1, S, 0, 256)
+        out_pairs(1, V, 256, HALF)
+        for i in range(2, 4):
+            pass2(i, 2)
+            pass2(i, 3)
+        finish_add(2)
+        out_pairs(2, S, 0, 256)
+        out_pairs(2, V, 256, HALF)
+        finish_add(3)
+        out_pairs(3, S, 0, 256)
+        out_pairs(3, V, 256, HALF)

@@ -7,8 +7,8 @@ B, HALF, MID = 512, 512, 2048
 FLOPS = 2 * B * MID * MID + 2 * B * MID * HALF
 
 P = 128
-TT = B // P
 NG = MID // 512
+NT = 256
 F32 = mybir.dt.float32
 BF16 = mybir.dt.bfloat16
 U8 = mybir.dt.uint8
@@ -19,11 +19,6 @@ FP8X4 = mybir.dt.float8_e4m3fn_x4
 FP4X4 = mybir.dt.float4_e2m1fn_x4
 ALU = mybir.AluOpType
 ACT = mybir.ActivationFunctionType
-
-NM = 3
-TILES = [(g, j) for g in range(NM) for j in range(4)]
-SWEEP = 6
-EXIT_V = (1, 3, 5, 7, 9)
 
 
 def tile_additivecoupling_pa_w4_kernel(
@@ -38,39 +33,25 @@ def tile_additivecoupling_pa_w4_kernel(
 
         ident = keep.tile([P, P], F32, name="ident")
         make_identity(nc, ident[:])
-        w4s = keep.tile([P, NG, MID], U8, name="w4s", align_bytes=64)
+        w4s = []
+        for part in range(2):
+            s_p = keep.tile([P, NG, 1024], U8, name=f"w4s{part}", align_bytes=64)
+            w4s.append(s_p)
         w5s = keep.tile([P, NG, HALF], U8, name="w5s", align_bytes=64)
-        warm = keep.tile([P, 1], F32, name="warm")
-        nc.vector.memset(warm[:], 0.0)
-        srows = keep.tile([P, P], F32, name="srows")
-        nc.vector.memset(srows[:], 0.0)
-        brows = keep.tile([P, P], BF16, name="brows")
-        nc.vector.memset(brows[:], 0.0)
-        nc.vector.memset(w4s[:].rearrange("p g n -> p (g n)").bitcast(I32), 0)
-        nc.gpsimd.memset(w5s[:].rearrange("p g n -> p (g n)").bitcast(I32), 0)
-        warm2 = keep.tile([P, 1], F32, name="warm2")
-        nc.scalar.activation(out=warm2[:], in_=warm[:], func=ACT.Relu)
+        b4f = keep.tile([P, P], F32, name="b4f")
+        nc.vector.memset(w4s[0][:].rearrange("p g n -> p (g n)").bitcast(I32), 0)
+        nc.vector.memset(b4f[:], 0.0)
+        nc.vector.memset(w4s[1][:].rearrange("p g n -> p (g n)").bitcast(I32), 0)
+        nc.vector.memset(w5s[:].rearrange("p g n -> p (g n)").bitcast(I32), 0)
 
-        h3v = h3_bytes.rearrange("(p i) k -> p i k", i=TT)
-        hb0 = keep.tile([P, TT, 512], U8, name="hb0", align_bytes=64)
-        hb1 = keep.tile([P, TT, 512], U8, name="hb1", align_bytes=64)
-        hb23 = keep.tile([P, TT, 1024], U8, name="hb23", align_bytes=64)
-        hb = [hb0, hb1, hb23[:, :, 0:512], hb23[:, :, 512:1024]]
-        sc, w4a = [], []
-        w4b = keep.tile([P, NG, 1024], U8, name="w4b", align_bytes=64)
-        w5 = keep.tile([P, NG, 1024], U8, name="w5", align_bytes=64)
-        for g in range(NG):
-            s_g = keep.tile([P, 512], F32, name=f"sc{g}", align_bytes=64)
-            sc.append(s_g)
-        w4a0 = keep.tile([P, 1024 * NM], U8, name="w4a0", align_bytes=64)
-        w4a1 = keep.tile([P, 1024 * NM], U8, name="w4a1", align_bytes=64)
-        w4a23 = keep.tile([P, 2, 1024 * NM], U8, name="w4a23", align_bytes=64)
-        w4a = [w4a0, w4a1, w4a23[:, 0, :], w4a23[:, 1, :]]
-        b4bc = keep.tile([P, 512], BF16, name="b4bc")
-        b5bc = keep.tile([P, HALF], BF16, name="b5bc")
+        h3v = h3_bytes.rearrange("(h p i) k -> h p i k", h=2, i=2)
+        hb = {}
 
-        def load_w4(g):
-            nc.sync.dma_start(out=w4a[g][:].bitcast(I32), in_=W4_words[g, :, 0 : 1024 * NM].bitcast(I32))
+        def load_h3(h, g0, g1):
+            t = keep.tile([P, 2, 512 * (g1 - g0)], U8, name=f"hb{h}_{g0}", align_bytes=64)
+            nc.sync.dma_start(out=t[:], in_=h3v[h, :, :, 512 * g0 : 512 * g1])
+            for g in range(g0, g1):
+                hb[h, g] = t[:, :, 512 * (g - g0) : 512 * (g - g0 + 1)]
 
         def load_scales(dst, src):
             for r in range(4):
@@ -78,315 +59,289 @@ def tile_additivecoupling_pa_w4_kernel(
                     out=dst[r:P:32, :, :].bitcast(I32), in_=src[:, r:16:4, :].rearrange("g q n -> q g n").bitcast(I32)
                 )
 
-        s0tile = keep.tile([P, 4], F32, name="s0tile")
-        with nc.allow_non_contiguous_dma(reason="512 scales, one to a partition and column"):
-            nc.sync.dma_start(out=s0tile[:], in_=h3_scale[:, 0:512].rearrange("o (m p) -> p (o m)", p=P))
-        nc.sync.dma_start(out=hb0[:], in_=h3v[:, :, 0:512])
-        nc.sync.dma_start(out=srows[0:16, :], in_=h3_scale.rearrange("o (c p) -> (o c) p", p=P))
-        nc.sync.dma_start(out=hb1[:], in_=h3v[:, :, 512:1024])
-        load_scales(w4s, W4_scales)
-        nc.sync.dma_start(out=hb23[:], in_=h3v[:, :, 1024:2048])
-        load_w4(0)
-        nc.sync.dma_start(out=brows[0:12, :], in_=b4[0 : 512 * NM].rearrange("(c p) -> c p", p=P))
-        load_w4(1)
-        nc.sync.dma_start(
-            out=w4a23[:].bitcast(I32), in_=W4_words[2:4, :, 0 : 1024 * NM].rearrange("g p n -> p g n").bitcast(I32)
-        )
-        nc.sync.dma_start(out=w4b[:].bitcast(I32), in_=W4_words[:, :, 1024 * NM :].rearrange("g p n -> p g n").bitcast(I32))
+        w4 = {}
+
+        def load_w4_group(g):
+            t = keep.tile([P, 2048], U8, name=f"w4a{g}", align_bytes=64)
+            nc.sync.dma_start(out=t[:].bitcast(I32), in_=W4_words[g, :, 0:2048].bitcast(I32))
+            for c in range(8):
+                w4[g, c] = t[:, 256 * c : 256 * (c + 1)]
+
+        def load_w4_channels(o):
+            t = keep.tile([P, NG, 1024], U8, name=f"w4b{o}", align_bytes=64)
+            nc.sync.dma_start(
+                out=t[:].bitcast(I32),
+                in_=W4_words[:, :, 1024 * o : 1024 * (o + 1)].rearrange("g p n -> p g n").bitcast(I32),
+            )
+            for g in range(NG):
+                for q in range(4):
+                    w4[g, 4 * o + q] = t[:, g, 256 * q : 256 * (q + 1)]
+
+        hs = keep.tile([P, NG, 4], F32, name="hs")
+        b4r = keep.tile([16, P], BF16, name="b4r")
+        w5 = keep.tile([P, NG, 1024], U8, name="w5", align_bytes=64)
+        b5bc = keep.tile([P, HALF], BF16, name="b5bc")
+        xv = x.rearrange("(h p i) c -> h p i c", h=2, i=2)
+        xt = []
+        for h in range(2):
+            x_h = keep.tile([P, 2, 2 * HALF], BF16, name=f"xt{h}")
+            xt.append(x_h)
+
+        load_h3(0, 0, 1)
+        nc.sync.dma_start(out=hs[:], in_=h3_scale.rearrange("o (g p t) -> p (o g) t", p=P, t=4))
+        load_h3(0, 1, 4)
+        load_scales(w4s[0], W4_scales[:, :, 0:1024])
+        load_w4_group(0)
+        load_w4_group(1)
+        load_h3(1, 0, 2)
+        nc.sync.dma_start(out=b4r[:], in_=b4.rearrange("(c p) -> c p", p=P))
+        load_w4_group(2)
+        load_w4_group(3)
+        load_h3(1, 2, 4)
+        load_scales(w4s[1], W4_scales[:, :, 1024:2048])
+        load_w4_channels(2)
+        load_w4_channels(3)
+        nc.sync.dma_start(out=xt[0][:], in_=xv[0])
+        nc.sync.dma_start(out=b5bc[:], in_=b5.partition_broadcast(P))
         load_scales(w5s, W5_scales)
         nc.sync.dma_start(out=w5[:].bitcast(I32), in_=W5_words.rearrange("g p n -> p g n").bitcast(I32))
-        xt = keep.tile([P, TT, 2 * HALF], BF16, name="xt")
-        nc.sync.dma_start(out=b5bc[:], in_=b5.partition_broadcast(P))
-        nc.sync.dma_start(out=xt[:], in_=x.rearrange("(p i) c -> p i c", i=TT))
-        nc.sync.dma_start(out=b4bc[:], in_=b4[512 * NM :].partition_broadcast(P))
+        nc.sync.dma_start(out=xt[1][:], in_=xv[1])
 
-        h3g, h3q, h3s, prods = [], [], [], {}
-        for g in range(NG):
-            t_g = work.tile([P, B, 4], BF16, name="h3g", tag="h3g", bufs=2, align_bytes=64)
-            q_g = keep.tile([P, B], U32, name=f"h3q{g}", align_bytes=64)
-            s_g = keep.tile([P, B], U8, name=f"h3s{g}", align_bytes=64)
-            h3g.append(t_g)
-            h3q.append(q_g)
-            h3s.append(s_g)
+        wide, turned, scaled, h3q, h3s = {}, {}, {}, {}, {}
 
-        def product(g, i):
-            t = work.tile([P, 512], BF16, name="prod", tag="prod", bufs=6, align_bytes=64)
-            nc.vector.tensor_tensor(out=t[:], in0=hb[g][:, i, :].bitcast(FP8), in1=sc[g][:], op=ALU.mult)
-            prods[g, i] = t
-
-        def transpose_pair(g, half):
-            bank = psum.tile([P, 2, 2, P], F32, name="tr", tag="tr", bufs=2)
-            for ii in range(2):
-                words = prods[g, 2 * half + ii][:].bitcast(F32)
-                for u in range(2):
-                    nc.tensor.transpose(bank[:, ii, u, :], words[:, u::2], ident[:])
-            dst = h3g[g][:, 256 * half : 256 * (half + 1), :].rearrange("p c t -> p (c t)").bitcast(F32)
-            nc.scalar.copy(
-                out=dst.rearrange("p (i m u) -> p i m u", i=2, u=2), in_=bank[:].rearrange("p i u m -> p i m u")
-            )
-
-        def quantise_h3(g):
-            cols = slice(0, B)
-            nc.vector.quantize_mx(
-                out=h3q[g][:, cols].bitcast(FP8X4),
-                scales=h3s[g][:, cols],
-                in_=h3g[g][:, cols, :].rearrange("p c t -> p (c t)"),
-            )
-
-        acc = {}
-
-        def pass1(n, g):
-            if g == 0:
-                bank = psum.tile([P, B], F32, name="acc", tag=f"b{n % 6}", bufs=1)
-                acc[n] = bank
-            c = 4 * TILES[n][0] + TILES[n][1]
-            w = w4a[g][:, 256 * c : 256 * (c + 1)]
-            nc.tensor.matmul_mx(
-                out=acc[n][:],
-                lhsT=w.bitcast(FP4X4),
-                lhsT_scale=w4s[:, g, P * c : P * (c + 1)],
-                rhs=h3q[g][:].bitcast(FP8X4),
-                rhs_scale=h3s[g][:],
-                start=(g == 0),
-                stop=(g == NG - 1),
-            )
-
-        h4n = []
-        for g in range(NM):
-            t_g = keep.tile([P, 4, B], BF16, name=f"h4n{g}", align_bytes=64)
-            h4n.append(t_g)
-
-        def exit1(n):
-            g, j = TILES[n]
-            c = 4 * g + j
-            h4 = work.tile([P, B], BF16, name="h4", tag="h4", bufs=12, align_bytes=64)
-            if n in EXIT_V:
-                nc.vector.tensor_scalar(
-                    out=h4[:], in0=acc[n][:], scalar1=bt[:, c : c + 1], scalar2=0.0, op0=ALU.add, op1=ALU.max
-                )
+        def widen(h, g):
+            t = work.tile([P, 2, 512], BF16, name="wide", tag="wide", bufs=4, align_bytes=64)
+            if (h, g) == (0, 0):
+                nc.vector.tensor_copy(out=t[:, 0, :], in_=hb[h, g][:, 0, :].bitcast(FP8))
+                nc.scalar.activation(out=t[:, 1, :], in_=hb[h, g][:, 1, :].bitcast(FP8), func=ACT.Copy)
             else:
-                nc.scalar.activation(out=h4[:], in_=acc[n][:], func=ACT.Relu, bias=bt[:, c : c + 1])
-            nc.sync.dma_start(out=h4n[g][32 * j : 32 * (j + 1), :, :].rearrange("a s c -> a (s c)"), in_=h4[:])
+                for i in range(2):
+                    nc.scalar.copy(out=t[:, i, :], in_=hb[h, g][:, i, :].bitcast(FP8))
+            wide[h, g] = t
 
-        h4q, h4s = [], []
-        for g in range(NG):
-            q_g = keep.tile([P, B], U32, name=f"h4q{g}", align_bytes=64)
-            s_g = keep.tile([P, B], U8, name=f"h4s{g}", align_bytes=64)
-            h4q.append(q_g)
-            h4s.append(s_g)
+        def turn(h, g, bank_name):
+            bank = psum.tile([P, 2, 2, P], F32, name="turned", tag=bank_name)
+            for i in range(2):
+                words = wide[h, g][:, i, :].bitcast(F32)
+                for u in range(2):
+                    nc.tensor.transpose(bank[:, u, i, :], words[:, u::2], ident[:])
+            turned[h, g] = bank
 
-        inter = {}
-
-        def interleave(g, copy, lo, hi):
-            if g not in inter:
-                t = work.tile([P, B, 4], BF16, name="h4i", tag="h4i", bufs=3, align_bytes=64)
-                inter[g] = t
-            copy(out=inter[g][:, lo:hi, :], in_=h4n[g][:, :, lo:hi].rearrange("p t c -> p c t"))
-
-        def quantise_h4(g, lo=0, hi=B):
-            nc.vector.quantize_mx(
-                out=h4q[g][:, lo:hi].bitcast(FP8X4),
-                scales=h4s[g][:, lo:hi],
-                in_=inter[g][:, lo:hi, :].rearrange("p c t -> p (c t)"),
-            )
-
-        h4t = {}
-
-        def group_tokens(i):
-            o = 3
-            bank = psum.tile([P, 512], F32, name="acc", tag=f"b{i % 2}", bufs=1)
-            cols = slice(P * i, P * (i + 1))
-            for g in range(NG):
-                nc.tensor.matmul_mx(
-                    out=bank[:],
-                    lhsT=h3q[g][:, cols].bitcast(FP8X4),
-                    lhsT_scale=h3s[g][:, cols],
-                    rhs=w4b[:, g, 1024 * (o - NM) : 1024 * (o - NM + 1)].bitcast(FP4X4),
-                    rhs_scale=w4s[:, g, 512 * o : 512 * (o + 1)],
-                    start=(g == 0),
-                    stop=(g == NG - 1),
-                )
-            return bank
-
-        def add_b4(i, bank):
-            t = work.tile([P, 512], BF16, name="h4t", tag="h4t", bufs=4, align_bytes=64)
-            order = "q (p u e) -> q u p e"
+        def scale(h, g):
+            t = work.tile([P, NT, 4], BF16, name="scaled", tag="scaled", bufs=3, align_bytes=64)
+            halves = turned[h, g][:].rearrange("p u i m -> p (u i m)").bitcast(BF16)
             nc.vector.tensor_tensor(
-                out=t[:].rearrange("q (u p e) -> q u p e", u=2, e=2),
-                in0=bank[:].rearrange(order, u=2, e=2),
-                in1=b4bc[:].rearrange(order, u=2, e=2),
-                op=ALU.add,
+                out=t[:].rearrange("p c (u e) -> p c u e", u=2),
+                in0=halves.rearrange("p (u c e) -> p c u e", u=2, e=2),
+                in1=hs[:, g, :].rearrange("p (u e) -> p u e", u=2).unsqueeze(1).to_broadcast([P, NT, 2, 2]),
+                op=ALU.mult,
             )
-            h4t[i] = t
+            scaled[h, g] = t
 
-        turned = {}
-
-        def turn_tokens(i):
-            bank = psum.tile([P, 2, P], F32, name="tr", tag="tr", bufs=2)
-            words = h4t[i][:].bitcast(F32)
-            for u in range(2):
-                nc.tensor.transpose(bank[:, u, :], words[:, P * u : P * (u + 1)], ident[:])
-            r = work.tile([P, P, 4], BF16, name="h4r", tag="h4r", bufs=4, align_bytes=64)
-            nc.scalar.activation(
-                out=r[:].rearrange("p m (u e) -> p m u e", u=2),
-                in_=bank[:].rearrange("p u m -> p (u m)").bitcast(BF16).rearrange("p (u m e) -> p m u e", u=2, e=2),
-                func=ACT.Relu,
-            )
-            turned[i] = r
-
-        def quantise_turned(i):
-            cols = slice(P * i, P * (i + 1))
+        def quantise(src, name):
+            width = src.shape[1]
+            codes = keep.tile([P, width], U32, name=name + "q", align_bytes=64)
+            plane = keep.tile([P, width], U8, name=name + "s", align_bytes=64)
             nc.vector.quantize_mx(
-                out=h4q[3][:, cols].bitcast(FP8X4),
-                scales=h4s[3][:, cols],
-                in_=turned[i][:].rearrange("p m t -> p (m t)"),
+                out=codes[:].bitcast(FP8X4), scales=plane[:], in_=src[:].rearrange("p c t -> p (c t)")
+            )
+            return codes, plane
+
+        def quantise_h3(h, g):
+            h3q[h, g], h3s[h, g] = quantise(scaled[h, g], f"h3_{h}{g}")
+
+        def pass1(dst, h, c, g, start, stop, cols=slice(0, NT)):
+            nc.tensor.matmul_mx(
+                out=dst,
+                lhsT=w4[g, c].bitcast(FP4X4),
+                lhsT_scale=w4s[c // 8][:, g, P * (c % 8) : P * (c % 8 + 1)],
+                rhs=h3q[h, g][:, cols].bitcast(FP8X4),
+                rhs_scale=h3s[h, g][:, cols],
+                start=start,
+                stop=stop,
             )
 
-        acc2 = {}
+        b4c = keep.tile([P, 16], F32, name="b4c")
 
-        def pass2(i, g):
+        def turn_b4(bank_name):
+            bank = psum.tile([P, P], F32, name="b4bank", tag=bank_name)
+            nc.tensor.transpose(bank[:], b4f[:], ident[:])
+            nc.scalar.copy(out=b4c[:], in_=bank[:, 0:16])
+
+        planes = {}
+
+        def relu_and_move(h, bank, chans, first=0):
+            n, width = len(chans), bank.shape[2]
+            st = work.tile([P, n, width], BF16, name="staged", tag=f"staged{n * width}", bufs=8, align_bytes=64)
+            for j, c in enumerate(chans):
+                nc.scalar.activation(out=st[:, j, :], in_=bank[:, j, :], func=ACT.Relu, bias=b4c[:, c : c + 1])
+            g, q = chans[0] // 4, chans[0] % 4
+            if q == 0:
+                t = keep.tile([P, 4, n, width], BF16, name=f"planes{h}{g}_{first}", align_bytes=64)
+                for j in range(n):
+                    planes[h, g + j, first] = (t, j)
+            t = planes[h, g, first][0]
+            nc.sync.dma_start(
+                out=t[32 * q : 32 * (q + 1)].rearrange("a t j c -> a (t j c)"), in_=st[:].rearrange("p j c -> p (j c)")
+            )
+
+        def channel_tiles(h, chans, bank_name, first=0, width=NT):
+            bank = psum.tile([P, len(chans), width], F32, name="acc", tag=bank_name)
+            for j, c in enumerate(chans):
+                for g in range(NG):
+                    pass1(bank[:, j, :], h, c, g, g == 0, g == NG - 1, slice(first, first + width))
+            relu_and_move(h, bank, chans, first)
+
+        inter, h4q, h4s = {}, {}, {}
+
+        def interleave(h, g, first=0):
+            src, j = planes[h, g, first]
+            width = src.shape[3]
+            t = work.tile([P, width, 4], BF16, name="inter", tag="inter", bufs=3, align_bytes=64)
+            nc.vector.tensor_copy(
+                out=t[:].rearrange("p (c i) t -> p c t i", i=4),
+                in_=src[:, :, j, :].rearrange("p t (c i) -> p c t i", i=4),
+            )
+            inter[h, g, first] = t
+
+        def quantise_h4(h, g, first=0):
+            codes, plane = quantise(inter[h, g, first], f"h4_{h}{g}_{first}")
+            for lo in range(0, codes.shape[1], P):
+                h4q[h, (first + lo) // P, g] = codes[:, lo : lo + P]
+                h4s[h, (first + lo) // P, g] = plane[:, lo : lo + P]
+
+        acc2, pair = {}, {}
+
+        def pass2(h, i, g, bank_name=None):
             if g == 0:
-                bank = psum.tile([P, HALF], F32, name="acc", tag=f"b{2 + i}", bufs=1)
-                acc2[i] = bank
-            cols = slice(P * i, P * (i + 1))
+                bank = psum.tile([P, HALF], F32, name="acc2", tag=bank_name)
+                acc2[h, i] = bank
             nc.tensor.matmul_mx(
-                out=acc2[i][:],
-                lhsT=h4q[g][:, cols].bitcast(FP8X4),
-                lhsT_scale=h4s[g][:, cols],
+                out=acc2[h, i][:],
+                lhsT=h4q[h, i, g].bitcast(FP8X4),
+                lhsT_scale=h4s[h, i, g],
                 rhs=w5[:, g, :].bitcast(FP4X4),
                 rhs_scale=w5s[:, g, :],
                 start=(g == 0),
                 stop=(g == NG - 1),
             )
 
-        outv = out.rearrange("(p i) c -> p i c", i=TT)
+        def x_pair(h, i):
+            t = keep.tile([P, 2, HALF], F32, name=f"pair{h}{i}")
+            nc.scalar.copy(out=t[:, 1, :], in_=xt[h][:, i, 1::2])
+            nc.vector.tensor_tensor(out=t[:, 0, :], in0=xt[h][:, i, 0::2], in1=b5bc[:], op=ALU.add)
+            pair[h, i] = t
 
-        outt = []
-        for i in range(TT):
-            o_i = keep.tile([P, HALF, 2], F32, name=f"o{i}")
-            outt.append(o_i)
+        outv = out.rearrange("(h p i) c -> h p i c", h=2, i=2)
 
-        def finish_add(i):
-            nc.vector.tensor_tensor(out=pair[:, i, 0, :], in0=acc2[i][:], in1=pair[:, i, 0, :], op=ALU.add)
+        def add_m(h, i):
+            nc.vector.tensor_tensor(out=pair[h, i][:, 0, :], in0=acc2[h, i][:], in1=pair[h, i][:, 0, :], op=ALU.add)
 
-        def out_pairs(i, copy, lo, hi):
-            copy(out=outt[i][:, lo:hi, :], in_=pair[:, i, :, lo:hi].rearrange("p r j -> p j r"))
-            start = 0 if i < 3 else lo
-            if hi == HALF or i == 3:
-                nc.sync.dma_start(
-                    out=outv[:, i, 2 * start : 2 * hi], in_=outt[i][:, start:hi, :].rearrange("p j r -> p (j r)")
-                )
+        def store(h, i, split, apart=False):
+            t = keep.tile([P, HALF, 2], F32, name=f"o{h}{i}")
+            parts = [(nc.vector.tensor_copy, split, HALF), (nc.scalar.copy, 0, split)]
+            for copy, lo, hi in parts:
+                if lo < hi:
+                    copy(out=t[:, lo:hi, :], in_=pair[h, i][:, :, lo:hi].rearrange("p r j -> p j r"))
+                if apart:
+                    nc.sync.dma_start(
+                        out=outv[h, :, i, 2 * lo : 2 * hi], in_=t[:, lo:hi, :].rearrange("p j r -> p (j r)")
+                    )
+            if not apart:
+                nc.sync.dma_start(out=outv[h, :, i, :], in_=t[:].rearrange("p j r -> p (j r)"))
 
-        def spread(bank, cols, first):
-            for m in range(4):
-                nc.tensor.transpose(bank[:, m, :], cols[:, first + m : first + m + 1].to_broadcast([P, P]), ident[:])
+        sweep = []
+        for q in range(4):
+            bank = psum.tile([P, 2, NT], F32, name="acc", tag=f"b{q}")
+            sweep.append(bank)
 
-        def scale_bank(g):
-            bank = psum.tile([P, 4, P], F32, name="acc", tag=f"b{g}", bufs=1)
-            if g == 0:
-                spread(bank, s0tile, 0)
-            else:
-                spread(bank, stile, 4 * g)
-            return bank
+        def sweep_passes(g):
+            for q in range(4):
+                for j in range(2):
+                    pass1(sweep[q][:, j, :], 0, 4 * j + q, g, g == 0 and j == 0, g == NG - 1 and j == 1)
 
-        def scale_copy(g, bank, copy):
-            copy(out=sc[g][:], in_=bank[:].rearrange("p m n -> p (m n)"))
+        units = [(h, g) for h in range(2) for g in range(NG)]
 
-        scale_copy(0, scale_bank(0), nc.vector.tensor_copy)
-        stile = keep.tile([P, 16], F32, name="stile")
-        sbank = psum.tile([P, P], F32, name="tr", tag="tr", bufs=2)
-        nc.tensor.transpose(sbank[:], srows[:], ident[:])
-        nc.scalar.copy(out=stile[:], in_=sbank[:, 0:16])
-        scale_copy(1, scale_bank(1), nc.scalar.copy)
-        bt = keep.tile([P, 12], F32, name="bt")
+        def turn_unit(n):
+            turn(*units[n], f"b{4 + n % 4}")
 
-        pair = keep.tile([P, TT, 2, HALF], F32, name="pair")
-
-        def x_pairs(i):
-            nc.scalar.activation(out=pair[:, i, 1, :], in_=xt[:, i, 1::2], func=ACT.Copy)
-            nc.vector.tensor_tensor(out=pair[:, i, 0, :], in0=xt[:, i, 0::2], in1=b5bc[:], op=ALU.add)
-
-        def turn_b4():
-            browsf = keep.tile([P, P], F32, name="browsf")
-            nc.gpsimd.tensor_copy(out=browsf[:], in_=brows[:])
-            bbank = psum.tile([P, P], F32, name="tr", tag="tr", bufs=2)
-            nc.tensor.transpose(bbank[:], browsf[:], ident[:])
-            nc.scalar.copy(out=bt[:], in_=bbank[:, 0:12])
-
-        for g in range(NG):
-            if g == 2:
-                turn_b4()
-            product(g, 0)
-            product(g, 1)
-            transpose_pair(g, 0)
-            product(g, 2)
-            product(g, 3)
-            if g > 0:
-                quantise_h3(g - 1)
-            transpose_pair(g, 1)
-            if g == 0:
-                for later in range(2, NG):
-                    scale_copy(later, scale_bank(later), nc.scalar.copy)
-            if g > 0:
-                for n in range(SWEEP):
-                    pass1(n, g - 1)
-        quantise_h3(NG - 1)
-        for n in range(SWEEP):
-            pass1(n, NG - 1)
-            exit1(n)
-        V, S = nc.vector.tensor_copy, nc.scalar.copy
-
-        for n in range(SWEEP, len(TILES)):
+        for n in range(3):
+            widen(*units[n])
+            turn_unit(n)
+        widen(*units[3])
+        scale(*units[0])
+        quantise_h3(*units[0])
+        scale(*units[1])
+        sweep_passes(0)
+        widen(*units[4])
+        turn_unit(3)
+        turn_unit(4)
+        quantise_h3(*units[1])
+        scale(*units[2])
+        widen(*units[5])
+        widen(*units[6])
+        sweep_passes(1)
+        nc.vector.tensor_copy(out=b4f[0:16, :], in_=b4r[:])
+        quantise_h3(*units[2])
+        scale(*units[3])
+        sweep_passes(2)
+        turn_unit(5)
+        turn_unit(6)
+        turn_b4("b7")
+        widen(*units[7])
+        scale(*units[4])
+        quantise_h3(*units[3])
+        sweep_passes(3)
+        turn_unit(7)
+        for q in range(4):
+            relu_and_move(0, sweep[q], [q, 4 + q])
+        for n in range(5, 8):
+            scale(*units[n])
+            quantise_h3(*units[n - 1])
+        quantise_h3(*units[7])
+        for q in range(4):
+            channel_tiles(0, [8 + q, 12 + q], f"b{q}")
+        for g in range(2):
+            interleave(0, g)
+        for g in range(2):
+            quantise_h4(0, g)
+        for q in range(4):
+            channel_tiles(1, [q, 4 + q], f"b{4 + q}")
+            if q < 2:
+                x_pair(0, q)
+        for g in range(2, 4):
+            interleave(0, g)
+        for g in range(2, 4):
+            quantise_h4(0, g)
+        for q in range(4):
+            channel_tiles(1, [8 + q], f"b{q}")
+            if q < 2:
+                x_pair(1, q)
+        for g in range(2):
+            interleave(1, g)
+        for g in range(2):
+            quantise_h4(1, g)
+        for i in range(2):
+            for q in range(4):
+                channel_tiles(1, [12 + q], f"b{4 + q}", P * i, P)
             for g in range(NG):
-                pass1(n, g)
-            exit1(n)
-            if n < SWEEP + TT:
-                x_pairs(n - SWEEP)
-            if n == 9:
-                interleave(0, V, 0, 256)
-                interleave(0, S, 256, B)
-        quantise_h4(0)
-        add_b4(0, group_tokens(0))
-        interleave(1, V, 0, 256)
-        interleave(1, S, 256, B)
-        add_b4(1, group_tokens(1))
-        quantise_h4(1)
-        add_b4(2, group_tokens(2))
-        turn_tokens(0)
-        turn_tokens(1)
-        b3 = group_tokens(3)
-        add_b4(3, b3)
-        interleave(2, V, 0, 256)
-        interleave(2, S, 256, 512)
-        for i in range(2):
-            pass2(i, 0)
-            pass2(i, 1)
-        turn_tokens(2)
-        turn_tokens(3)
-        quantise_h4(2, 0, 256)
-        quantise_turned(0)
-        quantise_turned(1)
-        quantise_h4(2, 256, 512)
-        for i in range(2):
-            pass2(i, 2)
-            pass2(i, 3)
-        for i in range(2, 4):
-            pass2(i, 0)
-            pass2(i, 1)
-        quantise_turned(2)
-        finish_add(0)
-        quantise_turned(3)
-        out_pairs(0, S, 0, 256)
-        out_pairs(0, V, 256, HALF)
-        finish_add(1)
-        out_pairs(1, S, 0, 256)
-        out_pairs(1, V, 256, HALF)
-        for i in range(2, 4):
-            pass2(i, 2)
-            pass2(i, 3)
-        finish_add(2)
-        out_pairs(2, S, 0, 256)
-        out_pairs(2, V, 256, HALF)
-        finish_add(3)
-        out_pairs(3, S, 0, 256)
-        out_pairs(3, V, 256, HALF)
+                pass2(0, i, g, f"b{i}")
+            if i == 0:
+                interleave(1, 2)
+                add_m(0, 0)
+                quantise_h4(1, 2)
+        store(0, 0, HALF)
+        interleave(1, 3, 0)
+        quantise_h4(1, 3, 0)
+        add_m(0, 1)
+        for g in range(NG):
+            pass2(1, 0, g, "b2")
+        interleave(1, 3, P)
+        store(0, 1, 256)
+        quantise_h4(1, 3, P)
+        for g in range(NG):
+            pass2(1, 1, g, "b3")
+        add_m(1, 0)
+        store(1, 0, 256)
+        add_m(1, 1)
+        store(1, 1, 256, True)

@@ -39,6 +39,8 @@ def tile_additivecoupling_pa_w4_kernel(
             w4s.append(s_p)
         w5s = keep.tile([P, NG, HALF], U8, name="w5s", align_bytes=64)
         b4f = keep.tile([P, P], F32, name="b4f")
+        idle = keep.tile([P, 512], BF16, name="idle")
+        nc.vector.memset(idle[:], 0.0)
         nc.vector.memset(w4s[0][:].rearrange("p g n -> p (g n)").bitcast(I32), 0)
         nc.vector.memset(b4f[:], 0.0)
         nc.vector.memset(w4s[1][:].rearrange("p g n -> p (g n)").bitcast(I32), 0)
@@ -251,9 +253,6 @@ def tile_additivecoupling_pa_w4_kernel(
                 nc.sync.dma_start(out=outv[h, :, i, :], in_=t[:].rearrange("p j r -> p (j r)"))
 
         sweep = []
-        for q in range(4):
-            bank = psum.tile([P, 2, NT], F32, name="acc", tag=f"b{q}")
-            sweep.append(bank)
 
         def sweep_passes(g):
             for q in range(4):
@@ -265,10 +264,20 @@ def tile_additivecoupling_pa_w4_kernel(
         def turn_unit(n):
             turn(*units[n], f"b{4 + n % 4}")
 
+        def warm_up(count):
+            bank = psum.tile([P, 512], F32, name="unread", tag="b0")
+            for n in range(count):
+                nc.tensor.matmul(out=bank[:], lhsT=idle[:, 0:P], rhs=idle[:], start=True, stop=True)
+
+        warm_counts = (5, 2, 1)
         for n in range(3):
             widen(*units[n])
+            warm_up(warm_counts[n])
             turn_unit(n)
         widen(*units[3])
+        for q in range(4):
+            bank = psum.tile([P, 2, NT], F32, name="acc", tag=f"b{q}")
+            sweep.append(bank)
         scale(*units[0])
         quantise_h3(*units[0])
         scale(*units[1])

@@ -38,11 +38,13 @@ def tile_additivecoupling_pa_w4_kernel(
             s_p = keep.tile([P, NG, 1024], U8, name=f"w4s{part}", align_bytes=64)
             w4s.append(s_p)
         w5s = keep.tile([P, NG, HALF], U8, name="w5s", align_bytes=64)
-        b4f = keep.tile([P, P], F32, name="b4f")
         idle = keep.tile([P, 512], BF16, name="idle")
+        rows = keep.tile([P, 512], BF16, name="rows")
+        identb = keep.tile([P, P], BF16, name="identb")
         nc.vector.memset(idle[:], 0.0)
+        nc.vector.memset(rows[:], 0.0)
         nc.vector.memset(w4s[0][:].rearrange("p g n -> p (g n)").bitcast(I32), 0)
-        nc.vector.memset(b4f[:], 0.0)
+        nc.vector.tensor_copy(out=identb[:], in_=ident[:])
         nc.vector.memset(w4s[1][:].rearrange("p g n -> p (g n)").bitcast(I32), 0)
         nc.vector.memset(w5s[:].rearrange("p g n -> p (g n)").bitcast(I32), 0)
 
@@ -66,8 +68,9 @@ def tile_additivecoupling_pa_w4_kernel(
         def load_w4_group(g):
             t = keep.tile([P, 2048], U8, name=f"w4a{g}", align_bytes=64)
             nc.sync.dma_start(out=t[:].bitcast(I32), in_=W4_words[g, :, 0:2048].bitcast(I32))
-            for c in range(8):
-                w4[g, c] = t[:, 256 * c : 256 * (c + 1)]
+            w4[g] = t
+
+        w4b = {}
 
         def load_w4_channels(o):
             t = keep.tile([P, NG, 1024], U8, name=f"w4b{o}", align_bytes=64)
@@ -75,36 +78,31 @@ def tile_additivecoupling_pa_w4_kernel(
                 out=t[:].bitcast(I32),
                 in_=W4_words[:, :, 1024 * o : 1024 * (o + 1)].rearrange("g p n -> p g n").bitcast(I32),
             )
-            for g in range(NG):
-                for q in range(4):
-                    w4[g, 4 * o + q] = t[:, g, 256 * q : 256 * (q + 1)]
+            w4b[o] = t
 
         hs = keep.tile([P, NG, 4], F32, name="hs")
-        b4r = keep.tile([16, P], BF16, name="b4r")
         w5 = keep.tile([P, NG, 1024], U8, name="w5", align_bytes=64)
-        b5bc = keep.tile([P, HALF], BF16, name="b5bc")
         xv = x.rearrange("(h p i) c -> h p i c", h=2, i=2)
         xt = []
         for h in range(2):
             x_h = keep.tile([P, 2, 2 * HALF], BF16, name=f"xt{h}")
             xt.append(x_h)
 
-        load_h3(0, 0, 1)
+        load_h3(0, 0, 2)
         nc.sync.dma_start(out=hs[:], in_=h3_scale.rearrange("o (g p t) -> p (o g) t", p=P, t=4))
-        load_h3(0, 1, 4)
         load_scales(w4s[0], W4_scales[:, :, 0:1024])
         load_w4_group(0)
+        nc.scalar.dma_start(out=rows[0:4, :], in_=b4.rearrange("(o n) -> o n", o=4))
+        nc.scalar.dma_start(out=rows[4:5, :], in_=b5.rearrange("(o n) -> o n", o=1))
+        load_h3(0, 2, 4)
         load_w4_group(1)
-        load_h3(1, 0, 2)
-        nc.sync.dma_start(out=b4r[:], in_=b4.rearrange("(c p) -> c p", p=P))
         load_w4_group(2)
+        load_h3(1, 0, 4)
         load_w4_group(3)
-        load_h3(1, 2, 4)
         load_scales(w4s[1], W4_scales[:, :, 1024:2048])
         load_w4_channels(2)
         load_w4_channels(3)
         nc.sync.dma_start(out=xt[0][:], in_=xv[0])
-        nc.sync.dma_start(out=b5bc[:], in_=b5.partition_broadcast(P))
         load_scales(w5s, W5_scales)
         nc.sync.dma_start(out=w5[:].bitcast(I32), in_=W5_words.rearrange("g p n -> p g n").bitcast(I32))
         nc.sync.dma_start(out=xt[1][:], in_=xv[1])
@@ -112,7 +110,7 @@ def tile_additivecoupling_pa_w4_kernel(
         wide, turned, scaled, h3q, h3s = {}, {}, {}, {}, {}
 
         def widen(h, g):
-            t = work.tile([P, 2, 512], BF16, name="wide", tag="wide", bufs=4, align_bytes=64)
+            t = work.tile([P, 2, 512], BF16, name="wide", tag="wide", bufs=6, align_bytes=64)
             if (h, g) == (0, 0):
                 nc.vector.tensor_copy(out=t[:, 0, :], in_=hb[h, g][:, 0, :].bitcast(FP8))
                 nc.scalar.activation(out=t[:, 1, :], in_=hb[h, g][:, 1, :].bitcast(FP8), func=ACT.Copy)
@@ -152,81 +150,147 @@ def tile_additivecoupling_pa_w4_kernel(
         def quantise_h3(h, g):
             h3q[h, g], h3s[h, g] = quantise(scaled[h, g], f"h3_{h}{g}")
 
-        def pass1(dst, h, c, g, start, stop, cols=slice(0, NT)):
+        b4c = keep.tile([P, 2, 4], F32, name="b4c")
+        b4bc = keep.tile([P, 2, 512], BF16, name="b4wide")
+        b5bc = keep.tile([P, HALF], BF16, name="b5wide")
+
+        def turn_b4(bank_name):
+            bank = psum.tile([P, 4, 2], F32, name="b4bank", tag=bank_name)
+            for q in range(4):
+                nc.tensor.matmul(
+                    out=bank[:, q, :], lhsT=rows[:, P * q : P * (q + 1)], rhs=identb[:, 0:2], start=True, stop=True
+                )
+            return bank
+
+        def spread_row(r, bank_name):
+            bank = psum.tile([P, 512], F32, name="rowbank", tag=bank_name)
+            nc.tensor.matmul(
+                out=bank[:], lhsT=identb[:, r : r + 1].to_broadcast([P, P]), rhs=rows[:], start=True, stop=True
+            )
+            return bank
+
+        def keep_b4_row(o, bank, copy):
+            copy(
+                out=b4bc[:, o - 2, :].rearrange("m (u p e) -> m u p e", u=2, e=2),
+                in_=bank[:].rearrange("m (p u e) -> m u p e", u=2, e=2),
+            )
+
+        def pass1(dst, h, c, g, start, stop):
             nc.tensor.matmul_mx(
                 out=dst,
-                lhsT=w4[g, c].bitcast(FP4X4),
-                lhsT_scale=w4s[c // 8][:, g, P * (c % 8) : P * (c % 8 + 1)],
-                rhs=h3q[h, g][:, cols].bitcast(FP8X4),
-                rhs_scale=h3s[h, g][:, cols],
+                lhsT=w4[g][:, 256 * c : 256 * (c + 1)].bitcast(FP4X4),
+                lhsT_scale=w4s[0][:, g, P * c : P * (c + 1)],
+                rhs=h3q[h, g][:].bitcast(FP8X4),
+                rhs_scale=h3s[h, g][:],
                 start=start,
                 stop=stop,
             )
 
-        b4c = keep.tile([P, 16], F32, name="b4c")
-
-        def turn_b4(bank_name):
-            bank = psum.tile([P, P], F32, name="b4bank", tag=bank_name)
-            nc.tensor.transpose(bank[:], b4f[:], ident[:])
-            nc.scalar.copy(out=b4c[:], in_=bank[:, 0:16])
-
         planes = {}
 
-        def relu_and_move(h, bank, chans, first=0):
-            n, width = len(chans), bank.shape[2]
-            st = work.tile([P, n, width], BF16, name="staged", tag=f"staged{n * width}", bufs=8, align_bytes=64)
-            for j, c in enumerate(chans):
-                nc.scalar.activation(out=st[:, j, :], in_=bank[:, j, :], func=ACT.Relu, bias=b4c[:, c : c + 1])
-            g, q = chans[0] // 4, chans[0] % 4
-            if q == 0:
-                t = keep.tile([P, 4, n, width], BF16, name=f"planes{h}{g}_{first}", align_bytes=64)
-                for j in range(n):
-                    planes[h, g + j, first] = (t, j)
-            t = planes[h, g, first][0]
+        def relu_and_move(h, bank, q):
+            st = work.tile([P, 2, NT], BF16, name="staged", tag="staged", bufs=8, align_bytes=64)
+            for j in range(2):
+                nc.scalar.activation(out=st[:, j, :], in_=bank[:, j, :], func=ACT.Relu, bias=b4c[:, j, q : q + 1])
+            if h not in planes:
+                t = keep.tile([P, 4, 2, NT], BF16, name=f"planes{h}", align_bytes=64)
+                planes[h] = t
             nc.sync.dma_start(
-                out=t[32 * q : 32 * (q + 1)].rearrange("a t j c -> a (t j c)"), in_=st[:].rearrange("p j c -> p (j c)")
+                out=planes[h][32 * q : 32 * (q + 1)].rearrange("a t j c -> a (t j c)"),
+                in_=st[:].rearrange("p j c -> p (j c)"),
             )
 
-        def channel_tiles(h, chans, bank_name, first=0, width=NT):
-            bank = psum.tile([P, len(chans), width], F32, name="acc", tag=bank_name)
-            for j, c in enumerate(chans):
+        def channel_tiles(h, q, bank_name):
+            bank = psum.tile([P, 2, NT], F32, name="acc", tag=bank_name)
+            for j in range(2):
                 for g in range(NG):
-                    pass1(bank[:, j, :], h, c, g, g == 0, g == NG - 1, slice(first, first + width))
-            relu_and_move(h, bank, chans, first)
+                    pass1(bank[:, j, :], h, 4 * j + q, g, g == 0, g == NG - 1)
+            relu_and_move(h, bank, q)
 
         inter, h4q, h4s = {}, {}, {}
 
-        def interleave(h, g, first=0):
-            src, j = planes[h, g, first]
-            width = src.shape[3]
-            t = work.tile([P, width, 4], BF16, name="inter", tag="inter", bufs=3, align_bytes=64)
+        def interleave(h, g):
+            t = work.tile([P, NT, 4], BF16, name="inter", tag="inter", bufs=2, align_bytes=64)
             nc.vector.tensor_copy(
                 out=t[:].rearrange("p (c i) t -> p c t i", i=4),
-                in_=src[:, :, j, :].rearrange("p t (c i) -> p c t i", i=4),
+                in_=planes[h][:, :, g, :].rearrange("p t (c i) -> p c t i", i=4),
             )
-            inter[h, g, first] = t
+            inter[h, g] = t
 
-        def quantise_h4(h, g, first=0):
-            codes, plane = quantise(inter[h, g, first], f"h4_{h}{g}_{first}")
-            for lo in range(0, codes.shape[1], P):
-                h4q[h, (first + lo) // P, g] = codes[:, lo : lo + P]
-                h4s[h, (first + lo) // P, g] = plane[:, lo : lo + P]
+        def quantise_moved(h, g):
+            codes, plane = quantise(inter[h, g], f"h4_{h}{g}")
+            for i in range(2):
+                h4q[h, i, g] = codes[:, P * i : P * (i + 1)]
+                h4s[h, i, g] = plane[:, P * i : P * (i + 1)]
+
+        summed, back, relud = {}, {}, {}
+
+        def token_tile(h, i, o, bank_name):
+            bank = psum.tile([P, 512], F32, name="acct", tag=bank_name)
+            cols = slice(P * i, P * (i + 1))
+            for g in range(NG):
+                nc.tensor.matmul_mx(
+                    out=bank[:],
+                    lhsT=h3q[h, g][:, cols].bitcast(FP8X4),
+                    lhsT_scale=h3s[h, g][:, cols],
+                    rhs=w4b[o][:, g, :].bitcast(FP4X4),
+                    rhs_scale=w4s[1][:, g, 512 * (o - 2) : 512 * (o - 1)],
+                    start=(g == 0),
+                    stop=(g == NG - 1),
+                )
+            summed[h, i, o] = bank
+
+        def add_b4(h, i, o):
+            t = work.tile([P, 2, P, 2], BF16, name="biased", tag="biased", bufs=4, align_bytes=64)
+            nc.vector.tensor_tensor(
+                out=t[:],
+                in0=summed[h, i, o][:].rearrange("m (p u e) -> m u p e", u=2, e=2),
+                in1=b4bc[:, o - 2, :].rearrange("m (u p e) -> m u p e", u=2, e=2),
+                op=ALU.add,
+            )
+            summed[h, i, o] = t
+
+        def turn_back(h, i, bank_name):
+            bank = psum.tile([P, 2, 2, P], F32, name="back", tag=bank_name)
+            for o in range(2, 4):
+                words = summed[h, i, o][:].rearrange("m u p e -> m (u p e)").bitcast(F32)
+                for u in range(2):
+                    nc.tensor.transpose(bank[:, u, o - 2, :], words[:, P * u : P * (u + 1)], ident[:])
+            back[h, i] = bank
+
+        def relu_back(h, i, groups):
+            n = len(groups)
+            t = work.tile([P, n * P, 4], BF16, name="relud", tag="relud", bufs=4, align_bytes=64)
+            halves = back[h, i][:].rearrange("p u o m -> p (u o m)").bitcast(BF16)
+            lo = P * (groups[0] - 2)
+            nc.scalar.activation(
+                out=t[:].rearrange("p c (u e) -> p c u e", u=2),
+                in_=halves.rearrange("p (u c e) -> p c u e", u=2, e=2)[:, lo : lo + n * P],
+                func=ACT.Relu,
+            )
+            relud[h, i, groups] = t
+
+        def quantise_back(h, i, groups):
+            codes, plane = quantise(relud[h, i, groups], f"h4_{h}{i}_{groups[0]}")
+            for n, g in enumerate(groups):
+                h4q[h, i, g] = codes[:, P * n : P * (n + 1)]
+                h4s[h, i, g] = plane[:, P * n : P * (n + 1)]
 
         acc2, pair = {}, {}
 
-        def pass2(h, i, g, bank_name=None):
-            if g == 0:
-                bank = psum.tile([P, HALF], F32, name="acc2", tag=bank_name)
-                acc2[h, i] = bank
-            nc.tensor.matmul_mx(
-                out=acc2[h, i][:],
-                lhsT=h4q[h, i, g].bitcast(FP8X4),
-                lhsT_scale=h4s[h, i, g],
-                rhs=w5[:, g, :].bitcast(FP4X4),
-                rhs_scale=w5s[:, g, :],
-                start=(g == 0),
-                stop=(g == NG - 1),
-            )
+        def stage2(h, i, bank_name):
+            bank = psum.tile([P, HALF], F32, name="acc2", tag=bank_name)
+            acc2[h, i] = bank
+            for g in range(NG):
+                nc.tensor.matmul_mx(
+                    out=bank[:],
+                    lhsT=h4q[h, i, g].bitcast(FP8X4),
+                    lhsT_scale=h4s[h, i, g],
+                    rhs=w5[:, g, :].bitcast(FP4X4),
+                    rhs_scale=w5s[:, g, :],
+                    start=(g == 0),
+                    stop=(g == NG - 1),
+                )
 
         def x_pair(h, i):
             t = keep.tile([P, 2, HALF], F32, name=f"pair{h}{i}")
@@ -269,11 +333,21 @@ def tile_additivecoupling_pa_w4_kernel(
             for n in range(count):
                 nc.tensor.matmul(out=bank[:], lhsT=idle[:, 0:P], rhs=idle[:], start=True, stop=True)
 
-        warm_counts = (5, 2, 1)
-        for n in range(3):
-            widen(*units[n])
-            warm_up(warm_counts[n])
-            turn_unit(n)
+        warm_up(4)
+        widen(*units[0])
+        row2 = spread_row(2, "b1")
+        row3 = spread_row(3, "b2")
+        columns = turn_b4("b3")
+        turn_unit(0)
+        widen(*units[1])
+        turn_unit(1)
+        keep_b4_row(3, row3, nc.vector.tensor_copy)
+        keep_b4_row(2, row2, nc.scalar.copy)
+        nc.scalar.copy(out=b4c[:], in_=columns[:].rearrange("p q j -> p j q"))
+        row5 = spread_row(4, "b6")
+        warm_up(2)
+        nc.scalar.copy(out=b5bc[:], in_=row5[:])
+        widen(*units[2])
         widen(*units[3])
         for q in range(4):
             bank = psum.tile([P, 2, NT], F32, name="acc", tag=f"b{q}")
@@ -282,74 +356,86 @@ def tile_additivecoupling_pa_w4_kernel(
         quantise_h3(*units[0])
         scale(*units[1])
         sweep_passes(0)
-        widen(*units[4])
+        turn_unit(2)
         turn_unit(3)
-        turn_unit(4)
         quantise_h3(*units[1])
         scale(*units[2])
-        widen(*units[5])
-        widen(*units[6])
+        for n in range(4, 8):
+            widen(*units[n])
         sweep_passes(1)
-        nc.vector.tensor_copy(out=b4f[0:16, :], in_=b4r[:])
+        turn_unit(4)
+        turn_unit(5)
         quantise_h3(*units[2])
         scale(*units[3])
         sweep_passes(2)
-        turn_unit(5)
-        turn_unit(6)
-        turn_b4("b7")
-        widen(*units[7])
-        scale(*units[4])
         quantise_h3(*units[3])
+        scale(*units[4])
         sweep_passes(3)
+        turn_unit(6)
         turn_unit(7)
         for q in range(4):
-            relu_and_move(0, sweep[q], [q, 4 + q])
-        for n in range(5, 8):
-            scale(*units[n])
-            quantise_h3(*units[n - 1])
+            relu_and_move(0, sweep[q], q)
+        scale(*units[5])
+        quantise_h3(*units[4])
+        token_tile(0, 0, 2, "b4")
+        token_tile(0, 0, 3, "b0")
+        scale(*units[6])
+        quantise_h3(*units[5])
+        token_tile(0, 1, 2, "b1")
+        scale(*units[7])
+        quantise_h3(*units[6])
+        token_tile(0, 1, 3, "b2")
+        add_b4(0, 0, 2)
         quantise_h3(*units[7])
-        for q in range(4):
-            channel_tiles(0, [8 + q, 12 + q], f"b{q}")
-        for g in range(2):
-            interleave(0, g)
-        for g in range(2):
-            quantise_h4(0, g)
-        for q in range(4):
-            channel_tiles(1, [q, 4 + q], f"b{4 + q}")
-            if q < 2:
-                x_pair(0, q)
-        for g in range(2, 4):
-            interleave(0, g)
-        for g in range(2, 4):
-            quantise_h4(0, g)
-        for q in range(4):
-            channel_tiles(1, [8 + q], f"b{q}")
-            if q < 2:
-                x_pair(1, q)
-        for g in range(2):
-            interleave(1, g)
-        for g in range(2):
-            quantise_h4(1, g)
+        add_b4(0, 0, 3)
+        add_b4(0, 1, 2)
+        add_b4(0, 1, 3)
         for i in range(2):
-            for q in range(4):
-                channel_tiles(1, [12 + q], f"b{4 + q}", P * i, P)
-            for g in range(NG):
-                pass2(0, i, g, f"b{i}")
-            if i == 0:
-                interleave(1, 2)
-                add_m(0, 0)
-                quantise_h4(1, 2)
+            x_pair(0, i)
+        channel_tiles(1, 0, "b3")
+        x_pair(1, 0)
+        channel_tiles(1, 1, "b5")
+        x_pair(1, 1)
+        channel_tiles(1, 2, "b6")
+        channel_tiles(1, 3, "b7")
+        turn_back(0, 0, "b4")
+        turn_back(0, 1, "b0")
+        for g in range(2):
+            interleave(0, g)
+        for g in range(2):
+            quantise_moved(0, g)
+        for i in range(2):
+            relu_back(0, i, (2, 3))
+        token_tile(1, 0, 2, "b1")
+        token_tile(1, 0, 3, "b2")
+        for i in range(2):
+            quantise_back(0, i, (2, 3))
+        add_b4(1, 0, 2)
+        add_b4(1, 0, 3)
+        stage2(0, 0, "b3")
+        token_tile(1, 1, 2, "b5")
+        turn_back(1, 0, "b6")
+        token_tile(1, 1, 3, "b7")
+        interleave(1, 0)
+        interleave(1, 1)
+        add_m(0, 0)
+        add_b4(1, 1, 2)
+        relu_back(1, 0, (2, 3))
+        quantise_moved(1, 0)
+        quantise_moved(1, 1)
+        add_b4(1, 1, 3)
         store(0, 0, HALF)
-        interleave(1, 3, 0)
-        quantise_h4(1, 3, 0)
+        stage2(0, 1, "b4")
+        turn_back(1, 1, "b0")
+        quantise_back(1, 0, (2, 3))
+        stage2(1, 0, "b1")
         add_m(0, 1)
-        for g in range(NG):
-            pass2(1, 0, g, "b2")
-        interleave(1, 3, P)
+        relu_back(1, 1, (2,))
+        relu_back(1, 1, (3,))
+        quantise_back(1, 1, (2,))
         store(0, 1, 256)
-        quantise_h4(1, 3, P)
-        for g in range(NG):
-            pass2(1, 1, g, "b3")
+        quantise_back(1, 1, (3,))
+        stage2(1, 1, "b2")
         add_m(1, 0)
         store(1, 0, 256)
         add_m(1, 1)

@@ -40,11 +40,13 @@ def tile_additivecoupling_pa_w4_kernel(
         w5s = keep.tile([P, NG, HALF], U8, name="w5s", align_bytes=64)
         idle = keep.tile([P, 512], BF16, name="idle")
         rows = keep.tile([P, 512], BF16, name="rows")
+        rows5 = keep.tile([P, 512], BF16, name="rows5")
         identb = keep.tile([P, P], BF16, name="identb")
         nc.vector.memset(idle[:], 0.0)
         nc.vector.memset(rows[:], 0.0)
         nc.vector.memset(w4s[0][:].rearrange("p g n -> p (g n)").bitcast(I32), 0)
         nc.vector.tensor_copy(out=identb[:], in_=ident[:])
+        nc.vector.memset(rows5[:], 0.0)
         nc.vector.memset(w4s[1][:].rearrange("p g n -> p (g n)").bitcast(I32), 0)
         nc.vector.memset(w5s[:].rearrange("p g n -> p (g n)").bitcast(I32), 0)
 
@@ -88,13 +90,15 @@ def tile_additivecoupling_pa_w4_kernel(
             x_h = keep.tile([P, 2, 2 * HALF], BF16, name=f"xt{h}")
             xt.append(x_h)
 
-        load_h3(0, 0, 2)
-        nc.sync.dma_start(out=hs[:], in_=h3_scale.rearrange("o (g p t) -> p (o g) t", p=P, t=4))
-        load_scales(w4s[0], W4_scales[:, :, 0:1024])
-        load_w4_group(0)
+        load_h3(0, 0, 1)
         nc.scalar.dma_start(out=rows[0:4, :], in_=b4.rearrange("(o n) -> o n", o=4))
-        nc.scalar.dma_start(out=rows[4:5, :], in_=b5.rearrange("(o n) -> o n", o=1))
+        nc.sync.dma_start(out=hs[:], in_=h3_scale.rearrange("o (g p t) -> p (o g) t", p=P, t=4))
+        load_scales(w4s[0][:, 0:1, :], W4_scales[0:1, :, 0:1024])
+        load_h3(0, 1, 2)
+        load_w4_group(0)
         load_h3(0, 2, 4)
+        nc.sync.dma_start(out=rows5[0:1, :], in_=b5.rearrange("(o n) -> o n", o=1))
+        load_scales(w4s[0][:, 1:4, :], W4_scales[1:4, :, 0:1024])
         load_w4_group(1)
         load_w4_group(2)
         load_h3(1, 0, 4)
@@ -108,47 +112,56 @@ def tile_additivecoupling_pa_w4_kernel(
         nc.sync.dma_start(out=xt[1][:], in_=xv[1])
 
         wide, turned, scaled, h3q, h3s = {}, {}, {}, {}, {}
+        for h in range(2):
+            for g in range(NG):
+                h3q[h, g] = keep.tile([P, NT], U32, name=f"h3q{h}{g}", align_bytes=64)
+                h3s[h, g] = keep.tile([P, NT], U8, name=f"h3s{h}{g}", align_bytes=64)
 
         def widen(h, g):
-            t = work.tile([P, 2, 512], BF16, name="wide", tag="wide", bufs=6, align_bytes=64)
-            if (h, g) == (0, 0):
-                nc.vector.tensor_copy(out=t[:, 0, :], in_=hb[h, g][:, 0, :].bitcast(FP8))
-                nc.scalar.activation(out=t[:, 1, :], in_=hb[h, g][:, 1, :].bitcast(FP8), func=ACT.Copy)
-            else:
-                for i in range(2):
-                    nc.scalar.copy(out=t[:, i, :], in_=hb[h, g][:, i, :].bitcast(FP8))
-            wide[h, g] = t
-
-        def turn(h, g, bank_name):
-            bank = psum.tile([P, 2, 2, P], F32, name="turned", tag=bank_name)
             for i in range(2):
-                words = wide[h, g][:, i, :].bitcast(F32)
-                for u in range(2):
-                    nc.tensor.transpose(bank[:, u, i, :], words[:, u::2], ident[:])
-            turned[h, g] = bank
+                t = work.tile([P, 512], BF16, name="wide", tag="wide", bufs=12, align_bytes=64)
+                src = hb[h, g][:, i, :].bitcast(FP8)
+                if (h, g) != (0, 0):
+                    nc.scalar.copy(out=t[:], in_=src)
+                elif i == 0:
+                    nc.vector.tensor_copy(out=t[:], in_=src)
+                else:
+                    nc.scalar.activation(out=t[:], in_=src, func=ACT.Copy)
+                wide[h, g, i] = t
 
-        def scale(h, g):
-            t = work.tile([P, NT, 4], BF16, name="scaled", tag="scaled", bufs=3, align_bytes=64)
-            halves = turned[h, g][:].rearrange("p u i m -> p (u i m)").bitcast(BF16)
+        def turn(h, g, tiles, bank_name):
+            bank = psum.tile([P, 2, len(tiles), P], F32, name="turned", tag=bank_name)
+            for n, i in enumerate(tiles):
+                words = wide[h, g, i][:].bitcast(F32)
+                for u in range(2):
+                    nc.tensor.transpose(bank[:, u, n, :], words[:, u::2], ident[:])
+            turned[h, g, tiles] = bank
+
+        def scale(h, g, tiles):
+            width = P * len(tiles)
+            t = work.tile([P, width, 4], BF16, name="scaled", tag="scaled", bufs=3, align_bytes=64)
+            halves = turned[h, g, tiles][:].rearrange("p u i m -> p (u i m)").bitcast(BF16)
             nc.vector.tensor_tensor(
                 out=t[:].rearrange("p c (u e) -> p c u e", u=2),
                 in0=halves.rearrange("p (u c e) -> p c u e", u=2, e=2),
-                in1=hs[:, g, :].rearrange("p (u e) -> p u e", u=2).unsqueeze(1).to_broadcast([P, NT, 2, 2]),
+                in1=hs[:, g, :].rearrange("p (u e) -> p u e", u=2).unsqueeze(1).to_broadcast([P, width, 2, 2]),
                 op=ALU.mult,
             )
-            scaled[h, g] = t
+            scaled[h, g, tiles] = t
+
+        def quantise_into(src, codes, plane):
+            nc.vector.quantize_mx(out=codes.bitcast(FP8X4), scales=plane, in_=src[:].rearrange("p c t -> p (c t)"))
 
         def quantise(src, name):
             width = src.shape[1]
             codes = keep.tile([P, width], U32, name=name + "q", align_bytes=64)
             plane = keep.tile([P, width], U8, name=name + "s", align_bytes=64)
-            nc.vector.quantize_mx(
-                out=codes[:].bitcast(FP8X4), scales=plane[:], in_=src[:].rearrange("p c t -> p (c t)")
-            )
+            quantise_into(src, codes[:], plane[:])
             return codes, plane
 
-        def quantise_h3(h, g):
-            h3q[h, g], h3s[h, g] = quantise(scaled[h, g], f"h3_{h}{g}")
+        def quantise_h3(h, g, tiles):
+            cols = slice(P * tiles[0], P * (tiles[-1] + 1))
+            quantise_into(scaled[h, g, tiles], h3q[h, g][:, cols], h3s[h, g][:, cols])
 
         b4c = keep.tile([P, 2, 4], F32, name="b4c")
         b4bc = keep.tile([P, 2, 512], BF16, name="b4wide")
@@ -162,10 +175,10 @@ def tile_additivecoupling_pa_w4_kernel(
                 )
             return bank
 
-        def spread_row(r, bank_name):
+        def spread_row(src, r, bank_name):
             bank = psum.tile([P, 512], F32, name="rowbank", tag=bank_name)
             nc.tensor.matmul(
-                out=bank[:], lhsT=identb[:, r : r + 1].to_broadcast([P, P]), rhs=rows[:], start=True, stop=True
+                out=bank[:], lhsT=identb[:, r : r + 1].to_broadcast([P, P]), rhs=src[:], start=True, stop=True
             )
             return bank
 
@@ -250,22 +263,20 @@ def tile_additivecoupling_pa_w4_kernel(
             )
             summed[h, i, o] = t
 
-        def turn_back(h, i, bank_name):
-            bank = psum.tile([P, 2, 2, P], F32, name="back", tag=bank_name)
-            for o in range(2, 4):
+        def turn_back(h, i, groups, bank_name):
+            bank = psum.tile([P, 2, len(groups), P], F32, name="back", tag=bank_name)
+            for n, o in enumerate(groups):
                 words = summed[h, i, o][:].rearrange("m u p e -> m (u p e)").bitcast(F32)
                 for u in range(2):
-                    nc.tensor.transpose(bank[:, u, o - 2, :], words[:, P * u : P * (u + 1)], ident[:])
-            back[h, i] = bank
+                    nc.tensor.transpose(bank[:, u, n, :], words[:, P * u : P * (u + 1)], ident[:])
+            back[h, i, groups] = bank
 
         def relu_back(h, i, groups):
-            n = len(groups)
-            t = work.tile([P, n * P, 4], BF16, name="relud", tag="relud", bufs=4, align_bytes=64)
-            halves = back[h, i][:].rearrange("p u o m -> p (u o m)").bitcast(BF16)
-            lo = P * (groups[0] - 2)
+            t = work.tile([P, len(groups) * P, 4], BF16, name="relud", tag="relud", bufs=4, align_bytes=64)
+            halves = back[h, i, groups][:].rearrange("p u o m -> p (u o m)").bitcast(BF16)
             nc.scalar.activation(
                 out=t[:].rearrange("p c (u e) -> p c u e", u=2),
-                in_=halves.rearrange("p (u c e) -> p c u e", u=2, e=2)[:, lo : lo + n * P],
+                in_=halves.rearrange("p (u c e) -> p c u e", u=2, e=2),
                 func=ACT.Relu,
             )
             relud[h, i, groups] = t
@@ -292,6 +303,25 @@ def tile_additivecoupling_pa_w4_kernel(
                     stop=(g == NG - 1),
                 )
 
+        def stage2_last(h, i, bank_names):
+            banks = []
+            for name in bank_names:
+                bank = psum.tile([P, 2, 256], F32, name="acc2z", tag=name)
+                nc.tensor.matmul(out=bank[:, 1, :], lhsT=idle[:, 0:P], rhs=idle[:, 0:256], start=True, stop=True)
+                banks.append(bank)
+            for g in range(NG):
+                for n, bank in enumerate(banks):
+                    nc.tensor.matmul_mx(
+                        out=bank[:, 0, :],
+                        lhsT=h4q[h, i, g].bitcast(FP8X4),
+                        lhsT_scale=h4s[h, i, g],
+                        rhs=w5[:, g, 512 * n : 512 * (n + 1)].bitcast(FP4X4),
+                        rhs_scale=w5s[:, g, 256 * n : 256 * (n + 1)],
+                        start=(g == 0),
+                        stop=(g == NG - 1),
+                    )
+            return banks
+
         def x_pair(h, i):
             t = keep.tile([P, 2, HALF], F32, name=f"pair{h}{i}")
             nc.scalar.copy(out=t[:, 1, :], in_=xt[h][:, i, 1::2])
@@ -303,18 +333,26 @@ def tile_additivecoupling_pa_w4_kernel(
         def add_m(h, i):
             nc.vector.tensor_tensor(out=pair[h, i][:, 0, :], in0=acc2[h, i][:], in1=pair[h, i][:, 0, :], op=ALU.add)
 
-        def store(h, i, split, apart=False):
+        def lay_side_by_side(h, i):
+            t = keep.tile([P, HALF, 2], F32, name="xb")
+            nc.scalar.copy(out=t[:], in_=pair[h, i][:].rearrange("p r j -> p j r"))
+            return t
+
+        def finish_last(h, i, banks, xb):
+            for n, bank in enumerate(banks):
+                t = keep.tile([P, 256, 2], F32, name=f"last{n}")
+                nc.vector.tensor_tensor(
+                    out=t[:], in0=bank[:].rearrange("p r j -> p j r"), in1=xb[:, 256 * n : 256 * (n + 1), :], op=ALU.add
+                )
+                nc.sync.dma_start(out=outv[h, :, i, 512 * n : 512 * (n + 1)], in_=t[:].rearrange("p j r -> p (j r)"))
+
+        def store(h, i, split):
             t = keep.tile([P, HALF, 2], F32, name=f"o{h}{i}")
             parts = [(nc.vector.tensor_copy, split, HALF), (nc.scalar.copy, 0, split)]
             for copy, lo, hi in parts:
                 if lo < hi:
                     copy(out=t[:, lo:hi, :], in_=pair[h, i][:, :, lo:hi].rearrange("p r j -> p j r"))
-                if apart:
-                    nc.sync.dma_start(
-                        out=outv[h, :, i, 2 * lo : 2 * hi], in_=t[:, lo:hi, :].rearrange("p j r -> p (j r)")
-                    )
-            if not apart:
-                nc.sync.dma_start(out=outv[h, :, i, :], in_=t[:].rearrange("p j r -> p (j r)"))
+            nc.sync.dma_start(out=outv[h, :, i, :], in_=t[:].rearrange("p j r -> p (j r)"))
 
         sweep = []
 
@@ -323,72 +361,69 @@ def tile_additivecoupling_pa_w4_kernel(
                 for j in range(2):
                     pass1(sweep[q][:, j, :], 0, 4 * j + q, g, g == 0 and j == 0, g == NG - 1 and j == 1)
 
-        units = [(h, g) for h in range(2) for g in range(NG)]
-
-        def turn_unit(n):
-            turn(*units[n], f"b{4 + n % 4}")
-
         def warm_up(count):
             bank = psum.tile([P, 512], F32, name="unread", tag="b0")
             for n in range(count):
                 nc.tensor.matmul(out=bank[:], lhsT=idle[:, 0:P], rhs=idle[:], start=True, stop=True)
 
+        both = (0, 1)
         warm_up(4)
-        widen(*units[0])
-        row2 = spread_row(2, "b1")
-        row3 = spread_row(3, "b2")
+        widen(0, 0)
+        row2 = spread_row(rows, 2, "b1")
+        turn(0, 0, (0,), "b4")
+        turn(0, 0, (1,), "b5")
+        row3 = spread_row(rows, 3, "b2")
         columns = turn_b4("b3")
-        turn_unit(0)
-        widen(*units[1])
-        turn_unit(1)
-        keep_b4_row(3, row3, nc.vector.tensor_copy)
         keep_b4_row(2, row2, nc.scalar.copy)
-        nc.scalar.copy(out=b4c[:], in_=columns[:].rearrange("p q j -> p j q"))
-        row5 = spread_row(4, "b6")
+        widen(0, 1)
         warm_up(2)
-        nc.scalar.copy(out=b5bc[:], in_=row5[:])
-        widen(*units[2])
-        widen(*units[3])
+        turn(0, 1, both, "b6")
+        keep_b4_row(3, row3, nc.scalar.copy)
+        nc.scalar.copy(out=b4c[:], in_=columns[:].rearrange("p q j -> p j q"))
+        widen(0, 2)
+        widen(0, 3)
         for q in range(4):
             bank = psum.tile([P, 2, NT], F32, name="acc", tag=f"b{q}")
             sweep.append(bank)
-        scale(*units[0])
-        quantise_h3(*units[0])
-        scale(*units[1])
+        scale(0, 0, (0,))
+        scale(0, 0, (1,))
+        quantise_h3(0, 0, (0,))
+        quantise_h3(0, 0, (1,))
+        scale(0, 1, both)
         sweep_passes(0)
-        turn_unit(2)
-        turn_unit(3)
-        quantise_h3(*units[1])
-        scale(*units[2])
-        for n in range(4, 8):
-            widen(*units[n])
+        turn(0, 2, both, "b7")
+        turn(0, 3, both, "b4")
+        quantise_h3(0, 1, both)
+        scale(0, 2, both)
         sweep_passes(1)
-        turn_unit(4)
-        turn_unit(5)
-        quantise_h3(*units[2])
-        scale(*units[3])
+        row5 = spread_row(rows5, 0, "b5")
+        widen(1, 0)
+        nc.scalar.copy(out=b5bc[:], in_=row5[:])
+        for g in range(1, NG):
+            widen(1, g)
+        quantise_h3(0, 2, both)
+        scale(0, 3, both)
         sweep_passes(2)
-        quantise_h3(*units[3])
-        scale(*units[4])
+        turn(1, 0, both, "b6")
+        turn(1, 1, both, "b5")
+        quantise_h3(0, 3, both)
+        scale(1, 0, both)
         sweep_passes(3)
-        turn_unit(6)
-        turn_unit(7)
+        turn(1, 2, both, "b7")
+        turn(1, 3, both, "b4")
         for q in range(4):
             relu_and_move(0, sweep[q], q)
-        scale(*units[5])
-        quantise_h3(*units[4])
-        token_tile(0, 0, 2, "b4")
-        token_tile(0, 0, 3, "b0")
-        scale(*units[6])
-        quantise_h3(*units[5])
-        token_tile(0, 1, 2, "b1")
-        scale(*units[7])
-        quantise_h3(*units[6])
+        for g in range(1, NG):
+            scale(1, g, both)
+            quantise_h3(1, g - 1, both)
+        token_tile(0, 0, 2, "b6")
+        token_tile(0, 1, 2, "b0")
+        token_tile(0, 0, 3, "b1")
         token_tile(0, 1, 3, "b2")
         add_b4(0, 0, 2)
-        quantise_h3(*units[7])
-        add_b4(0, 0, 3)
+        quantise_h3(1, NG - 1, both)
         add_b4(0, 1, 2)
+        add_b4(0, 0, 3)
         add_b4(0, 1, 3)
         for i in range(2):
             x_pair(0, i)
@@ -396,47 +431,48 @@ def tile_additivecoupling_pa_w4_kernel(
         x_pair(1, 0)
         channel_tiles(1, 1, "b5")
         x_pair(1, 1)
-        channel_tiles(1, 2, "b6")
-        channel_tiles(1, 3, "b7")
-        turn_back(0, 0, "b4")
-        turn_back(0, 1, "b0")
+        channel_tiles(1, 2, "b7")
+        channel_tiles(1, 3, "b4")
+        turn_back(0, 0, (2, 3), "b6")
+        turn_back(0, 1, (2, 3), "b0")
         for g in range(2):
             interleave(0, g)
         for g in range(2):
             quantise_moved(0, g)
         for i in range(2):
             relu_back(0, i, (2, 3))
+        xb = lay_side_by_side(1, 1)
         token_tile(1, 0, 2, "b1")
-        token_tile(1, 0, 3, "b2")
-        for i in range(2):
-            quantise_back(0, i, (2, 3))
+        token_tile(1, 1, 2, "b2")
+        token_tile(1, 0, 3, "b3")
+        quantise_back(0, 0, (2, 3))
         add_b4(1, 0, 2)
-        add_b4(1, 0, 3)
-        stage2(0, 0, "b3")
-        token_tile(1, 1, 2, "b5")
-        turn_back(1, 0, "b6")
-        token_tile(1, 1, 3, "b7")
-        interleave(1, 0)
-        interleave(1, 1)
-        add_m(0, 0)
+        quantise_back(0, 1, (2, 3))
         add_b4(1, 1, 2)
+        interleave(1, 0)
+        add_b4(1, 0, 3)
+        stage2(0, 0, "b5")
+        turn_back(1, 0, (2, 3), "b7")
+        turn_back(1, 1, (2,), "b4")
+        stage2(0, 1, "b6")
+        token_tile(1, 1, 3, "b0")
+        add_m(0, 0)
+        interleave(1, 1)
         relu_back(1, 0, (2, 3))
         quantise_moved(1, 0)
         quantise_moved(1, 1)
-        add_b4(1, 1, 3)
-        store(0, 0, HALF)
-        stage2(0, 1, "b4")
-        turn_back(1, 1, "b0")
         quantise_back(1, 0, (2, 3))
-        stage2(1, 0, "b1")
-        add_m(0, 1)
+        store(0, 0, 256)
         relu_back(1, 1, (2,))
-        relu_back(1, 1, (3,))
+        add_m(0, 1)
+        add_b4(1, 1, 3)
+        stage2(1, 0, "b1")
+        turn_back(1, 1, (3,), "b2")
         quantise_back(1, 1, (2,))
         store(0, 1, 256)
-        quantise_back(1, 1, (3,))
-        stage2(1, 1, "b2")
+        relu_back(1, 1, (3,))
         add_m(1, 0)
+        quantise_back(1, 1, (3,))
+        last = stage2_last(1, 1, ("b3", "b7"))
         store(1, 0, 256)
-        add_m(1, 1)
-        store(1, 1, 256, True)
+        finish_last(1, 1, last, xb)

@@ -361,13 +361,7 @@ def tile_additivecoupling_pa_w4_kernel(
                 for j in range(2):
                     pass1(sweep[q][:, j, :], 0, 4 * j + q, g, g == 0 and j == 0, g == NG - 1 and j == 1)
 
-        def warm_up(count):
-            bank = psum.tile([P, 512], F32, name="unread", tag="b0")
-            for n in range(count):
-                nc.tensor.matmul(out=bank[:], lhsT=idle[:, 0:P], rhs=idle[:], start=True, stop=True)
-
         both = (0, 1)
-        warm_up(4)
         widen(0, 0)
         row2 = spread_row(rows, 2, "b1")
         turn(0, 0, (0,), "b4")
@@ -376,7 +370,6 @@ def tile_additivecoupling_pa_w4_kernel(
         columns = turn_b4("b3")
         keep_b4_row(2, row2, nc.scalar.copy)
         widen(0, 1)
-        warm_up(2)
         turn(0, 1, both, "b6")
         keep_b4_row(3, row3, nc.scalar.copy)
         nc.scalar.copy(out=b4c[:], in_=columns[:].rearrange("p q j -> p j q"))

@@ -40,13 +40,11 @@ def tile_additivecoupling_pa_w4_kernel(
         w5s = keep.tile([P, NG, HALF], U8, name="w5s", align_bytes=64)
         idle = keep.tile([P, 512], BF16, name="idle")
         rows = keep.tile([P, 512], BF16, name="rows")
-        rows5 = keep.tile([P, 512], BF16, name="rows5")
         identb = keep.tile([P, P], BF16, name="identb")
         nc.vector.memset(idle[:], 0.0)
         nc.vector.memset(rows[:], 0.0)
         nc.vector.memset(w4s[0][:].rearrange("p g n -> p (g n)").bitcast(I32), 0)
         nc.vector.tensor_copy(out=identb[:], in_=ident[:])
-        nc.vector.memset(rows5[:], 0.0)
         nc.vector.memset(w4s[1][:].rearrange("p g n -> p (g n)").bitcast(I32), 0)
         nc.vector.memset(w5s[:].rearrange("p g n -> p (g n)").bitcast(I32), 0)
 
@@ -97,7 +95,6 @@ def tile_additivecoupling_pa_w4_kernel(
         load_h3(0, 1, 2)
         load_w4_group(0)
         load_h3(0, 2, 4)
-        nc.sync.dma_start(out=rows5[0:1, :], in_=b5.rearrange("(o n) -> o n", o=1))
         load_scales(w4s[0][:, 1:4, :], W4_scales[1:4, :, 0:1024])
         load_w4_group(1)
         load_w4_group(2)
@@ -107,6 +104,8 @@ def tile_additivecoupling_pa_w4_kernel(
         load_w4_channels(2)
         load_w4_channels(3)
         nc.sync.dma_start(out=xt[0][:], in_=xv[0])
+        b5bc = keep.tile([P, HALF], BF16, name="b5bc")
+        nc.sync.dma_start(out=b5bc[:], in_=b5.partition_broadcast(P))
         load_scales(w5s, W5_scales)
         nc.sync.dma_start(out=w5[:].bitcast(I32), in_=W5_words.rearrange("g p n -> p g n").bitcast(I32))
         nc.sync.dma_start(out=xt[1][:], in_=xv[1])
@@ -165,7 +164,6 @@ def tile_additivecoupling_pa_w4_kernel(
 
         b4c = keep.tile([P, 2, 4], F32, name="b4c")
         b4bc = keep.tile([P, 2, 512], BF16, name="b4wide")
-        b5bc = keep.tile([P, HALF], BF16, name="b5wide")
 
         def turn_b4(bank_name):
             bank = psum.tile([P, 4, 2], F32, name="b4bank", tag=bank_name)
@@ -221,6 +219,11 @@ def tile_additivecoupling_pa_w4_kernel(
             relu_and_move(h, bank, q)
 
         inter, h4q, h4s = {}, {}, {}
+
+        def interleave_on_scalar(h, g):
+            t = work.tile([P, NT, 4], BF16, name="inter", tag="inter", bufs=2, align_bytes=64)
+            nc.scalar.copy(out=t[:], in_=planes[h][:, :, g, :].rearrange("p t c -> p c t"))
+            inter[h, g] = t
 
         def interleave(h, g):
             t = work.tile([P, NT, 4], BF16, name="inter", tag="inter", bufs=2, align_bytes=64)
@@ -389,9 +392,7 @@ def tile_additivecoupling_pa_w4_kernel(
         quantise_h3(0, 1, both)
         scale(0, 2, both)
         sweep_passes(1)
-        row5 = spread_row(rows5, 0, "b5")
         widen(1, 0)
-        nc.scalar.copy(out=b5bc[:], in_=row5[:])
         for g in range(1, NG):
             widen(1, g)
         quantise_h3(0, 2, both)
@@ -413,8 +414,8 @@ def tile_additivecoupling_pa_w4_kernel(
         token_tile(0, 1, 2, "b0")
         token_tile(0, 0, 3, "b1")
         token_tile(0, 1, 3, "b2")
-        add_b4(0, 0, 2)
         quantise_h3(1, NG - 1, both)
+        add_b4(0, 0, 2)
         add_b4(0, 1, 2)
         add_b4(0, 0, 3)
         add_b4(0, 1, 3)
@@ -442,7 +443,7 @@ def tile_additivecoupling_pa_w4_kernel(
         add_b4(1, 0, 2)
         quantise_back(0, 1, (2, 3))
         add_b4(1, 1, 2)
-        interleave(1, 0)
+        interleave_on_scalar(1, 0)
         add_b4(1, 0, 3)
         stage2(0, 0, "b5")
         turn_back(1, 0, (2, 3), "b7")
@@ -455,7 +456,7 @@ def tile_additivecoupling_pa_w4_kernel(
         quantise_moved(1, 0)
         quantise_moved(1, 1)
         quantise_back(1, 0, (2, 3))
-        store(0, 0, 256)
+        store(0, 0, HALF)
         relu_back(1, 1, (2,))
         add_m(0, 1)
         add_b4(1, 1, 3)

@@ -364,7 +364,13 @@ def tile_additivecoupling_pa_w4_kernel(
                 for j in range(2):
                     pass1(sweep[q][:, j, :], 0, 4 * j + q, g, g == 0 and j == 0, g == NG - 1 and j == 1)
 
+        def warm_up(count):
+            bank = psum.tile([P, 512], F32, name="unread", tag="b0")
+            for n in range(count):
+                nc.tensor.matmul(out=bank[:], lhsT=idle[:, 0:P], rhs=idle[:], start=True, stop=True)
+
         both = (0, 1)
+        warm_up(4)
         widen(0, 0)
         row2 = spread_row(rows, 2, "b1")
         turn(0, 0, (0,), "b4")
@@ -373,6 +379,7 @@ def tile_additivecoupling_pa_w4_kernel(
         columns = turn_b4("b3")
         keep_b4_row(2, row2, nc.scalar.copy)
         widen(0, 1)
+        warm_up(2)
         turn(0, 1, both, "b6")
         keep_b4_row(3, row3, nc.scalar.copy)
         nc.scalar.copy(out=b4c[:], in_=columns[:].rearrange("p q j -> p j q"))

@@ -31,6 +31,8 @@ def tile_additivecoupling_pa_w4_kernel(
         psum = ctx.enter_context(tc.psum_pool(name="psum", bufs=1))
         ctx.enter_context(tc.manual_schedule())
 
+        rows = keep.tile([P, P], BF16, name="rows")
+        nc.gpsimd.memset(rows[:], 0.0)
         ident = keep.tile([P, P], F32, name="ident")
         make_identity(nc, ident[:])
         w4s = []
@@ -38,22 +40,20 @@ def tile_additivecoupling_pa_w4_kernel(
             s_p = keep.tile([P, NG, 1024], U8, name=f"w4s{part}", align_bytes=64)
             w4s.append(s_p)
         w5s = keep.tile([P, NG, HALF], U8, name="w5s", align_bytes=64)
-        idle = keep.tile([P, 512], BF16, name="idle")
-        rows = keep.tile([P, 512], BF16, name="rows")
+        zeros = keep.tile([P, 512], BF16, name="zeros")
         identb = keep.tile([P, P], BF16, name="identb")
-        nc.vector.memset(idle[:], 0.0)
-        nc.vector.memset(rows[:], 0.0)
+        nc.vector.memset(zeros[:], 0.0)
         nc.vector.memset(w4s[0][:].rearrange("p g n -> p (g n)").bitcast(I32), 0)
         nc.vector.tensor_copy(out=identb[:], in_=ident[:])
         nc.vector.memset(w4s[1][:].rearrange("p g n -> p (g n)").bitcast(I32), 0)
         nc.vector.memset(w5s[:].rearrange("p g n -> p (g n)").bitcast(I32), 0)
 
-        h3v = h3_bytes.rearrange("(h p i) k -> h p i k", h=2, i=2)
         hb = {}
 
         def load_h3(h, g0, g1):
             t = keep.tile([P, 2, 512 * (g1 - g0)], U8, name=f"hb{h}_{g0}", align_bytes=64)
-            nc.sync.dma_start(out=t[:], in_=h3v[h, :, :, 512 * g0 : 512 * g1])
+            src = h3_bytes.rearrange("(h p i) k -> h p i k", h=2, i=2)
+            nc.sync.dma_start(out=t[:], in_=src[h, :, :, 512 * g0 : 512 * g1])
             for g in range(g0, g1):
                 hb[h, g] = t[:, :, 512 * (g - g0) : 512 * (g - g0 + 1)]
 
@@ -82,6 +82,7 @@ def tile_additivecoupling_pa_w4_kernel(
 
         hs = keep.tile([P, NG, 4], F32, name="hs")
         w5 = keep.tile([P, NG, 1024], U8, name="w5", align_bytes=64)
+        b5bc = keep.tile([P, HALF], BF16, name="b5bc")
         xv = x.rearrange("(h p i) c -> h p i c", h=2, i=2)
         xt = []
         for h in range(2):
@@ -89,101 +90,118 @@ def tile_additivecoupling_pa_w4_kernel(
             xt.append(x_h)
 
         load_h3(0, 0, 1)
-        nc.scalar.dma_start(out=rows[0:4, :], in_=b4.rearrange("(o n) -> o n", o=4))
-        nc.sync.dma_start(out=hs[:], in_=h3_scale.rearrange("o (g p t) -> p (o g) t", p=P, t=4))
-        load_scales(w4s[0][:, 0:1, :], W4_scales[0:1, :, 0:1024])
+        nc.scalar.dma_start(out=rows[0:16, :], in_=b4.rearrange("(c n) -> c n", c=16))
         load_h3(0, 1, 2)
-        load_w4_group(0)
+        nc.sync.dma_start(out=hs[:], in_=h3_scale.rearrange("o (g p t) -> p (o g) t", p=P, t=4))
         load_h3(0, 2, 4)
+        load_scales(w4s[0][:, 0:1, :], W4_scales[0:1, :, 0:1024])
+        load_w4_group(0)
+        load_h3(1, 0, 2)
         load_scales(w4s[0][:, 1:4, :], W4_scales[1:4, :, 0:1024])
         load_w4_group(1)
+        load_h3(1, 2, 4)
         load_w4_group(2)
-        load_h3(1, 0, 4)
         load_w4_group(3)
         load_scales(w4s[1], W4_scales[:, :, 1024:2048])
         load_w4_channels(2)
         load_w4_channels(3)
         nc.sync.dma_start(out=xt[0][:], in_=xv[0])
-        b5bc = keep.tile([P, HALF], BF16, name="b5bc")
         nc.sync.dma_start(out=b5bc[:], in_=b5.partition_broadcast(P))
-        load_scales(w5s, W5_scales)
-        nc.sync.dma_start(out=w5[:].bitcast(I32), in_=W5_words.rearrange("g p n -> p g n").bitcast(I32))
-        nc.sync.dma_start(out=xt[1][:], in_=xv[1])
 
-        wide, turned, scaled, h3q, h3s = {}, {}, {}, {}, {}
+        def load_late():
+            nc.sync.dma_start(out=xt[1][:], in_=xv[1])
+            load_scales(w5s, W5_scales)
+            nc.sync.dma_start(out=w5[:].bitcast(I32), in_=W5_words.rearrange("g p n -> p g n").bitcast(I32))
+
+        wide, ordered, turned, scaled, h3q, h3s = {}, {}, {}, {}, {}, {}
         for h in range(2):
             for g in range(NG):
                 h3q[h, g] = keep.tile([P, NT], U32, name=f"h3q{h}{g}", align_bytes=64)
                 h3s[h, g] = keep.tile([P, NT], U8, name=f"h3s{h}{g}", align_bytes=64)
 
-        def widen(h, g):
-            for i in range(2):
-                t = work.tile([P, 512], BF16, name="wide", tag="wide", bufs=12, align_bytes=64)
-                src = hb[h, g][:, i, :].bitcast(FP8)
-                if (h, g) != (0, 0):
-                    nc.scalar.copy(out=t[:], in_=src)
-                elif i == 0:
-                    nc.vector.tensor_copy(out=t[:], in_=src)
-                else:
-                    nc.scalar.activation(out=t[:], in_=src, func=ACT.Copy)
-                wide[h, g, i] = t
+        def by_activation(out, in_):
+            nc.scalar.activation(out=out, in_=in_, func=ACT.Copy)
+
+        def widen(h, g, i, copy):
+            t = work.tile([P, 512], BF16, name="wide", tag="wide", bufs=16, align_bytes=64)
+            copy(out=t[:], in_=hb[h, g][:, i, :].bitcast(FP8))
+            wide[h, g, i] = t
+
+        def sort_words(h, g, i):
+            t = work.tile([P, 2, P], F32, name="ordered", tag="ordered", bufs=8, align_bytes=64)
+            nc.scalar.copy(out=t[:], in_=wide[h, g, i][:].bitcast(F32).rearrange("m (p u) -> m u p", u=2))
+            ordered[h, g, i] = t
 
         def turn(h, g, tiles, bank_name):
             bank = psum.tile([P, 2, len(tiles), P], F32, name="turned", tag=bank_name)
             for n, i in enumerate(tiles):
-                words = wide[h, g, i][:].bitcast(F32)
                 for u in range(2):
-                    nc.tensor.transpose(bank[:, u, n, :], words[:, u::2], ident[:])
-            turned[h, g, tiles] = bank
+                    if (h, g, i) in ordered:
+                        words = ordered[h, g, i][:, u, :]
+                    else:
+                        words = wide[h, g, i][:].bitcast(F32)[:, u::2]
+                    nc.tensor.transpose(bank[:, u, n, :], words, ident[:])
+                turned[h, g, i] = bank[:, :, n, :]
+            turned[h, g] = bank
 
-        def scale(h, g, tiles):
-            width = P * len(tiles)
-            t = work.tile([P, width, 4], BF16, name="scaled", tag="scaled", bufs=3, align_bytes=64)
-            halves = turned[h, g, tiles][:].rearrange("p u i m -> p (u i m)").bitcast(BF16)
+        def scale_into(dst, words, g, width):
             nc.vector.tensor_tensor(
-                out=t[:].rearrange("p c (u e) -> p c u e", u=2),
-                in0=halves.rearrange("p (u c e) -> p c u e", u=2, e=2),
+                out=dst.rearrange("p c (u e) -> p c u e", u=2),
+                in0=words.bitcast(BF16).rearrange("p u (c e) -> p c u e", e=2),
                 in1=hs[:, g, :].rearrange("p (u e) -> p u e", u=2).unsqueeze(1).to_broadcast([P, width, 2, 2]),
                 op=ALU.mult,
             )
-            scaled[h, g, tiles] = t
+
+        def scaled_tile(h, g):
+            if (h, g) not in scaled:
+                t = work.tile([P, NT, 4], BF16, name="scaled", tag="scaled", bufs=3, align_bytes=64)
+                scaled[h, g] = t
+            return scaled[h, g]
+
+        def scale(h, g):
+            scale_into(scaled_tile(h, g)[:], turned[h, g][:].rearrange("p u i m -> p u (i m)"), g, NT)
+
+        def scale_tile(h, g, i):
+            scale_into(scaled_tile(h, g)[:, P * i : P * (i + 1), :], turned[h, g, i], g, P)
 
         def quantise_into(src, codes, plane):
-            nc.vector.quantize_mx(out=codes.bitcast(FP8X4), scales=plane, in_=src[:].rearrange("p c t -> p (c t)"))
+            nc.vector.quantize_mx(out=codes.bitcast(FP8X4), scales=plane, in_=src.rearrange("p c t -> p (c t)"))
 
         def quantise(src, name):
             width = src.shape[1]
             codes = keep.tile([P, width], U32, name=name + "q", align_bytes=64)
             plane = keep.tile([P, width], U8, name=name + "s", align_bytes=64)
-            quantise_into(src, codes[:], plane[:])
+            quantise_into(src[:], codes[:], plane[:])
             return codes, plane
 
-        def quantise_h3(h, g, tiles):
-            cols = slice(P * tiles[0], P * (tiles[-1] + 1))
-            quantise_into(scaled[h, g, tiles], h3q[h, g][:, cols], h3s[h, g][:, cols])
+        def quantise_h3(h, g):
+            quantise_into(scaled[h, g][:], h3q[h, g][:], h3s[h, g][:])
 
-        b4c = keep.tile([P, 2, 4], F32, name="b4c")
-        b4bc = keep.tile([P, 2, 512], BF16, name="b4wide")
+        def quantise_h3_tile(h, g, i):
+            cols = slice(P * i, P * (i + 1))
+            quantise_into(scaled[h, g][:, cols, :], h3q[h, g][:, cols], h3s[h, g][:, cols])
+
+        b4c = keep.tile([P, 8], F32, name="b4c")
+        b4bc = keep.tile([P, 2, 512], BF16, name="b4bc")
 
         def turn_b4(bank_name):
-            bank = psum.tile([P, 4, 2], F32, name="b4bank", tag=bank_name)
-            for q in range(4):
-                nc.tensor.matmul(
-                    out=bank[:, q, :], lhsT=rows[:, P * q : P * (q + 1)], rhs=identb[:, 0:2], start=True, stop=True
-                )
+            bank = psum.tile([P, P], BF16, name="b4bank", tag=bank_name)
+            nc.tensor.transpose(bank[:], rows[:], identb[:])
             return bank
 
-        def spread_row(src, r, bank_name):
-            bank = psum.tile([P, 512], F32, name="rowbank", tag=bank_name)
-            nc.tensor.matmul(
-                out=bank[:], lhsT=identb[:, r : r + 1].to_broadcast([P, P]), rhs=src[:], start=True, stop=True
-            )
+        def spread_b4(o, bank_name):
+            bank = psum.tile([P, 4, P], F32, name="rowbank", tag=bank_name)
+            for n in range(4):
+                r = 4 * o + n
+                nc.tensor.matmul(
+                    out=bank[:, n, :], lhsT=identb[:, r : r + 1].to_broadcast([P, P]), rhs=rows[:], start=True, stop=True
+                )
             return bank
 
         def keep_b4_row(o, bank, copy):
             copy(
                 out=b4bc[:, o - 2, :].rearrange("m (u p e) -> m u p e", u=2, e=2),
-                in_=bank[:].rearrange("m (p u e) -> m u p e", u=2, e=2),
+                in_=bank[:].rearrange("m n c -> m (n c)").rearrange("m (p u e) -> m u p e", u=2, e=2),
             )
 
         def pass1(dst, h, c, g, start, stop):
@@ -202,7 +220,8 @@ def tile_additivecoupling_pa_w4_kernel(
         def relu_and_move(h, bank, q):
             st = work.tile([P, 2, NT], BF16, name="staged", tag="staged", bufs=8, align_bytes=64)
             for j in range(2):
-                nc.scalar.activation(out=st[:, j, :], in_=bank[:, j, :], func=ACT.Relu, bias=b4c[:, j, q : q + 1])
+                c = 4 * j + q
+                nc.scalar.activation(out=st[:, j, :], in_=bank[:, j, :], func=ACT.Relu, bias=b4c[:, c : c + 1])
             if h not in planes:
                 t = keep.tile([P, 4, 2, NT], BF16, name=f"planes{h}", align_bytes=64)
                 planes[h] = t
@@ -211,12 +230,17 @@ def tile_additivecoupling_pa_w4_kernel(
                 in_=st[:].rearrange("p j c -> p (j c)"),
             )
 
+        summed_c = {}
+
         def channel_tiles(h, q, bank_name):
             bank = psum.tile([P, 2, NT], F32, name="acc", tag=bank_name)
             for j in range(2):
                 for g in range(NG):
                     pass1(bank[:, j, :], h, 4 * j + q, g, g == 0, g == NG - 1)
-            relu_and_move(h, bank, q)
+            summed_c[h, q] = bank
+
+        def relu_move(h, q):
+            relu_and_move(h, summed_c[h, q], q)
 
         inter, h4q, h4s = {}, {}, {}
 
@@ -306,12 +330,15 @@ def tile_additivecoupling_pa_w4_kernel(
                     stop=(g == NG - 1),
                 )
 
-        def stage2_last(h, i, bank_names):
+        def zero_banks(bank_names):
             banks = []
             for name in bank_names:
                 bank = psum.tile([P, 2, 256], F32, name="acc2z", tag=name)
-                nc.tensor.matmul(out=bank[:, 1, :], lhsT=idle[:, 0:P], rhs=idle[:, 0:256], start=True, stop=True)
+                nc.tensor.matmul(out=bank[:, 1, :], lhsT=zeros[:, 0:P], rhs=zeros[:, 0:256], start=True, stop=True)
                 banks.append(bank)
+            return banks
+
+        def stage2_last(h, i, banks):
             for g in range(NG):
                 for n, bank in enumerate(banks):
                     nc.tensor.matmul_mx(
@@ -323,13 +350,16 @@ def tile_additivecoupling_pa_w4_kernel(
                         start=(g == 0),
                         stop=(g == NG - 1),
                     )
-            return banks
 
-        def x_pair(h, i):
-            t = keep.tile([P, 2, HALF], F32, name=f"pair{h}{i}")
-            nc.scalar.copy(out=t[:, 1, :], in_=xt[h][:, i, 1::2])
-            nc.vector.tensor_tensor(out=t[:, 0, :], in0=xt[h][:, i, 0::2], in1=b5bc[:], op=ALU.add)
-            pair[h, i] = t
+        for h in range(2):
+            for i in range(2):
+                pair[h, i] = keep.tile([P, 2, HALF], F32, name=f"pair{h}{i}")
+
+        def x_odd(h, i):
+            nc.scalar.copy(out=pair[h, i][:, 1, :], in_=xt[h][:, i, 1::2])
+
+        def x_even(h, i):
+            nc.vector.tensor_tensor(out=pair[h, i][:, 0, :], in0=xt[h][:, i, 0::2], in1=b5bc[:], op=ALU.add)
 
         outv = out.rearrange("(h p i) c -> h p i c", h=2, i=2)
 
@@ -357,123 +387,135 @@ def tile_additivecoupling_pa_w4_kernel(
                     copy(out=t[:, lo:hi, :], in_=pair[h, i][:, :, lo:hi].rearrange("p r j -> p j r"))
             nc.sync.dma_start(out=outv[h, :, i, :], in_=t[:].rearrange("p j r -> p (j r)"))
 
-        sweep = []
-
         def sweep_passes(g):
             for q in range(4):
                 for j in range(2):
-                    pass1(sweep[q][:, j, :], 0, 4 * j + q, g, g == 0 and j == 0, g == NG - 1 and j == 1)
+                    pass1(summed_c[0, q][:, j, :], 0, 4 * j + q, g, g == 0 and j == 0, g == NG - 1 and j == 1)
 
         def warm_up(count):
             bank = psum.tile([P, 512], F32, name="unread", tag="b0")
             for n in range(count):
-                nc.tensor.matmul(out=bank[:], lhsT=idle[:, 0:P], rhs=idle[:], start=True, stop=True)
+                nc.tensor.matmul(out=bank[:], lhsT=zeros[:, 0:P], rhs=zeros[:], start=True, stop=True)
 
-        both = (0, 1)
-        warm_up(4)
-        widen(0, 0)
-        row2 = spread_row(rows, 2, "b1")
+        warm_up(3)
+        spread = [spread_b4(o, f"b{o - 1}") for o in (2, 3)]
+        for i in range(2):
+            widen(0, 0, i, nc.vector.tensor_copy)
+        keep_b4_row(2, spread[0], by_activation)
+        widen(0, 1, 0, nc.scalar.copy)
+        widen(0, 1, 1, nc.vector.tensor_copy)
+        keep_b4_row(3, spread[1], nc.scalar.copy)
         turn(0, 0, (0,), "b4")
         turn(0, 0, (1,), "b5")
-        row3 = spread_row(rows, 3, "b2")
         columns = turn_b4("b3")
-        keep_b4_row(2, row2, nc.scalar.copy)
-        widen(0, 1)
+        turn(0, 1, (0, 1), "b6")
         warm_up(2)
-        turn(0, 1, both, "b6")
-        keep_b4_row(3, row3, nc.scalar.copy)
-        nc.scalar.copy(out=b4c[:], in_=columns[:].rearrange("p q j -> p j q"))
-        widen(0, 2)
-        widen(0, 3)
+        for g in (2, 3):
+            for i in range(2):
+                widen(0, g, i, nc.scalar.copy)
+        turn(0, 2, (0, 1), "b7")
+        nc.scalar.copy(out=b4c[:], in_=columns[:, 0:8])
+        for g in range(NG):
+            for i in range(2):
+                widen(1, g, i, nc.scalar.copy)
+            for i in range(2):
+                sort_words(1, g, i)
         for q in range(4):
-            bank = psum.tile([P, 2, NT], F32, name="acc", tag=f"b{q}")
-            sweep.append(bank)
-        scale(0, 0, (0,))
-        scale(0, 0, (1,))
-        quantise_h3(0, 0, (0,))
-        quantise_h3(0, 0, (1,))
-        scale(0, 1, both)
+            summed_c[0, q] = psum.tile([P, 2, NT], F32, name="acc", tag=f"b{q}")
+        scale_tile(0, 0, 0)
+        turn(0, 3, (0, 1), "b4")
+        scale_tile(0, 0, 1)
+        quantise_h3_tile(0, 0, 0)
+        quantise_h3_tile(0, 0, 1)
         sweep_passes(0)
-        turn(0, 2, both, "b7")
-        turn(0, 3, both, "b4")
-        quantise_h3(0, 1, both)
-        scale(0, 2, both)
+        turn(1, 0, (0, 1), "b5")
+        scale(0, 1)
+        turn(1, 1, (0, 1), "b6")
+        scale_tile(0, 2, 0)
+        quantise_h3(0, 1)
         sweep_passes(1)
-        widen(1, 0)
-        for g in range(1, NG):
-            widen(1, g)
-        quantise_h3(0, 2, both)
-        scale(0, 3, both)
+        scale_tile(0, 2, 1)
+        scale_tile(0, 3, 0)
+        quantise_h3(0, 2)
         sweep_passes(2)
-        turn(1, 0, both, "b6")
-        turn(1, 1, both, "b5")
-        quantise_h3(0, 3, both)
-        scale(1, 0, both)
+        turn(1, 2, (0, 1), "b7")
+        scale_tile(0, 3, 1)
+        turn(1, 3, (0, 1), "b4")
+        scale(1, 0)
+        quantise_h3(0, 3)
         sweep_passes(3)
-        turn(1, 2, both, "b7")
-        turn(1, 3, both, "b4")
         for q in range(4):
-            relu_and_move(0, sweep[q], q)
+            relu_move(0, q)
+        load_late()
         for g in range(1, NG):
-            scale(1, g, both)
-            quantise_h3(1, g - 1, both)
-        token_tile(0, 0, 2, "b6")
-        token_tile(0, 1, 2, "b0")
-        token_tile(0, 0, 3, "b1")
-        token_tile(0, 1, 3, "b2")
-        quantise_h3(1, NG - 1, both)
+            scale(1, g)
+            quantise_h3(1, g - 1)
+        token_tile(0, 0, 2, "b5")
+        token_tile(0, 1, 2, "b6")
+        token_tile(0, 0, 3, "b7")
+        token_tile(0, 1, 3, "b4")
         add_b4(0, 0, 2)
-        add_b4(0, 1, 2)
+        quantise_h3(1, NG - 1)
         add_b4(0, 0, 3)
+        add_b4(0, 1, 2)
         add_b4(0, 1, 3)
         for i in range(2):
-            x_pair(0, i)
-        channel_tiles(1, 0, "b3")
-        x_pair(1, 0)
-        channel_tiles(1, 1, "b5")
-        x_pair(1, 1)
-        channel_tiles(1, 2, "b7")
-        channel_tiles(1, 3, "b4")
-        turn_back(0, 0, (2, 3), "b6")
-        turn_back(0, 1, (2, 3), "b0")
-        for g in range(2):
-            interleave(0, g)
+            x_odd(0, i)
+        interleave_on_scalar(0, 0)
+        x_odd(1, 1)
+        channel_tiles(1, 0, "b0")
+        relu_move(1, 0)
+        x_even(1, 1)
+        interleave(0, 1)
+        x_even(0, 0)
         for g in range(2):
             quantise_moved(0, g)
-        for i in range(2):
-            relu_back(0, i, (2, 3))
+        channel_tiles(1, 1, "b1")
+        turn_back(0, 0, (2, 3), "b2")
+        turn_back(0, 1, (2, 3), "b3")
+        x_odd(1, 0)
+        relu_move(1, 1)
+        relu_back(0, 0, (2, 3))
         xb = lay_side_by_side(1, 1)
-        token_tile(1, 0, 2, "b1")
-        token_tile(1, 1, 2, "b2")
-        token_tile(1, 0, 3, "b3")
         quantise_back(0, 0, (2, 3))
-        add_b4(1, 0, 2)
-        quantise_back(0, 1, (2, 3))
-        add_b4(1, 1, 2)
-        interleave_on_scalar(1, 0)
-        add_b4(1, 0, 3)
-        stage2(0, 0, "b5")
-        turn_back(1, 0, (2, 3), "b7")
-        turn_back(1, 1, (2,), "b4")
-        stage2(0, 1, "b6")
-        token_tile(1, 1, 3, "b0")
+        x_even(0, 1)
+        x_even(1, 0)
+        channel_tiles(1, 2, "b5")
+        relu_move(1, 2)
+        channel_tiles(1, 3, "b6")
+        relu_move(1, 3)
+        relu_back(0, 1, (2, 3))
+        stage2(0, 0, "b7")
+        token_tile(1, 0, 2, "b0")
+        token_tile(1, 0, 3, "b2")
         add_m(0, 0)
-        interleave(1, 1)
-        relu_back(1, 0, (2, 3))
-        quantise_moved(1, 0)
-        quantise_moved(1, 1)
-        quantise_back(1, 0, (2, 3))
         store(0, 0, HALF)
-        relu_back(1, 1, (2,))
+        quantise_back(0, 1, (2, 3))
+        stage2(0, 1, "b4")
+        add_b4(1, 0, 2)
+        add_b4(1, 0, 3)
+        interleave_on_scalar(1, 0)
+        interleave(1, 1)
+        turn_back(1, 0, (2, 3), "b1")
+        token_tile(1, 1, 2, "b3")
+        token_tile(1, 1, 3, "b6")
         add_m(0, 1)
+        relu_back(1, 0, (2, 3))
+        store(0, 1, HALF)
+        quantise_moved(1, 1)
+        quantise_moved(1, 0)
+        add_b4(1, 1, 2)
+        quantise_back(1, 0, (2, 3))
+        turn_back(1, 1, (2,), "b7")
         add_b4(1, 1, 3)
-        stage2(1, 0, "b1")
-        turn_back(1, 1, (3,), "b2")
+        stage2(1, 0, "b0")
+        relu_back(1, 1, (2,))
+        turn_back(1, 1, (3,), "b4")
+        last = zero_banks(("b2", "b5"))
         quantise_back(1, 1, (2,))
-        store(0, 1, 256)
         relu_back(1, 1, (3,))
         add_m(1, 0)
         quantise_back(1, 1, (3,))
-        last = stage2_last(1, 1, ("b3", "b7"))
+        stage2_last(1, 1, last)
         store(1, 0, 256)
         finish_last(1, 1, last, xb)

@@ -42,7 +42,9 @@ def tile_additivecoupling_pa_w4_kernel(
         w5s = keep.tile([P, NG, HALF], U8, name="w5s", align_bytes=64)
         zeros = keep.tile([P, 512], BF16, name="zeros")
         identb = keep.tile([P, P], BF16, name="identb")
+        ones = keep.tile([P, 1], F32, name="ones")
         nc.vector.memset(zeros[:], 0.0)
+        nc.vector.memset(ones[:], 1.0)
         nc.vector.memset(w4s[0][:].rearrange("p g n -> p (g n)").bitcast(I32), 0)
         nc.vector.tensor_copy(out=identb[:], in_=ident[:])
         nc.vector.memset(w4s[1][:].rearrange("p g n -> p (g n)").bitcast(I32), 0)
@@ -127,9 +129,15 @@ def tile_additivecoupling_pa_w4_kernel(
             copy(out=t[:], in_=hb[h, g][:, i, :].bitcast(FP8))
             wide[h, g, i] = t
 
-        def sort_words(h, g, i):
+        def widen_sorted(h, g, i):
             t = work.tile([P, 2, P], F32, name="ordered", tag="ordered", bufs=8, align_bytes=64)
-            nc.scalar.copy(out=t[:], in_=wide[h, g, i][:].bitcast(F32).rearrange("m (p u) -> m u p", u=2))
+            nc.vector.tensor_scalar(
+                out=t[:].rearrange("m u p -> m (u p)").bitcast(BF16).rearrange("m (u p e) -> m p u e", u=2, e=2),
+                in0=hb[h, g][:, i, :].bitcast(FP8).rearrange("m (p u e) -> m p u e", u=2, e=2),
+                scalar1=ones[:],
+                scalar2=None,
+                op0=ALU.mult,
+            )
             ordered[h, g, i] = t
 
         def turn(h, g, tiles, bank_name):
@@ -399,41 +407,39 @@ def tile_additivecoupling_pa_w4_kernel(
 
         warm_up(3)
         spread = [spread_b4(o, f"b{o - 1}") for o in (2, 3)]
-        for i in range(2):
-            widen(0, 0, i, nc.vector.tensor_copy)
+        for g in range(2):
+            for i in range(2):
+                widen_sorted(0, g, i)
         keep_b4_row(2, spread[0], by_activation)
-        widen(0, 1, 0, nc.scalar.copy)
-        widen(0, 1, 1, nc.vector.tensor_copy)
         keep_b4_row(3, spread[1], nc.scalar.copy)
         turn(0, 0, (0,), "b4")
         turn(0, 0, (1,), "b5")
         columns = turn_b4("b3")
         turn(0, 1, (0, 1), "b6")
         warm_up(2)
-        for g in (2, 3):
-            for i in range(2):
-                widen(0, g, i, nc.scalar.copy)
-        turn(0, 2, (0, 1), "b7")
+        for i in range(2):
+            widen(0, 2, i, nc.scalar.copy)
         nc.scalar.copy(out=b4c[:], in_=columns[:, 0:8])
+        turn(0, 2, (0, 1), "b7")
+        for i in range(2):
+            widen(0, 3, i, nc.scalar.copy)
         for g in range(NG):
             for i in range(2):
                 widen(1, g, i, nc.scalar.copy)
-            for i in range(2):
-                sort_words(1, g, i)
         for q in range(4):
             summed_c[0, q] = psum.tile([P, 2, NT], F32, name="acc", tag=f"b{q}")
         scale_tile(0, 0, 0)
-        turn(0, 3, (0, 1), "b4")
         scale_tile(0, 0, 1)
         quantise_h3_tile(0, 0, 0)
         quantise_h3_tile(0, 0, 1)
         sweep_passes(0)
-        turn(1, 0, (0, 1), "b5")
+        turn(0, 3, (0, 1), "b4")
         scale(0, 1)
-        turn(1, 1, (0, 1), "b6")
         scale_tile(0, 2, 0)
         quantise_h3(0, 1)
         sweep_passes(1)
+        turn(1, 0, (0, 1), "b5")
+        turn(1, 1, (0, 1), "b6")
         scale_tile(0, 2, 1)
         scale_tile(0, 3, 0)
         quantise_h3(0, 2)
@@ -476,10 +482,9 @@ def tile_additivecoupling_pa_w4_kernel(
         x_odd(1, 0)
         relu_move(1, 1)
         relu_back(0, 0, (2, 3))
-        xb = lay_side_by_side(1, 1)
-        quantise_back(0, 0, (2, 3))
         x_even(0, 1)
         x_even(1, 0)
+        quantise_back(0, 0, (2, 3))
         channel_tiles(1, 2, "b5")
         relu_move(1, 2)
         channel_tiles(1, 3, "b6")
@@ -489,6 +494,7 @@ def tile_additivecoupling_pa_w4_kernel(
         token_tile(1, 0, 2, "b0")
         token_tile(1, 0, 3, "b2")
         add_m(0, 0)
+        xb = lay_side_by_side(1, 1)
         store(0, 0, HALF)
         quantise_back(0, 1, (2, 3))
         stage2(0, 1, "b4")

@@ -59,28 +59,28 @@ def tile_additivecoupling_pa_w4_kernel(
             for g in range(g0, g1):
                 hb[h, g] = t[:, :, 512 * (g - g0) : 512 * (g - g0 + 1)]
 
-        def load_scales(dst, src):
+        def load_scales(queue, dst, src):
             for r in range(4):
-                nc.sync.dma_start(
+                queue.dma_start(
                     out=dst[r:P:32, :, :].bitcast(I32), in_=src[:, r:16:4, :].rearrange("g q n -> q g n").bitcast(I32)
                 )
 
         w4 = {}
 
-        def load_w4_group(g):
-            t = keep.tile([P, 2048], U8, name=f"w4a{g}", align_bytes=64)
-            nc.sync.dma_start(out=t[:].bitcast(I32), in_=W4_words[g, :, 0:2048].bitcast(I32))
-            w4[g] = t
+        def load_w4_groups(g0, g1):
+            t = keep.tile([P, g1 - g0, 2048], U8, name=f"w4a{g0}", align_bytes=64)
+            nc.sync.dma_start(
+                out=t[:].bitcast(I32), in_=W4_words[g0:g1, :, 0:2048].rearrange("g p n -> p g n").bitcast(I32)
+            )
+            for g in range(g0, g1):
+                w4[g] = t[:, g - g0, :]
 
         w4b = {}
 
-        def load_w4_channels(o):
-            t = keep.tile([P, NG, 1024], U8, name=f"w4b{o}", align_bytes=64)
-            nc.sync.dma_start(
-                out=t[:].bitcast(I32),
-                in_=W4_words[:, :, 1024 * o : 1024 * (o + 1)].rearrange("g p n -> p g n").bitcast(I32),
-            )
-            w4b[o] = t
+        def load_w4_upper(g):
+            t = keep.tile([P, 2048], U8, name=f"w4b{g}", align_bytes=64)
+            nc.sync.dma_start(out=t[:].bitcast(I32), in_=W4_words[g, :, 2048:4096].bitcast(I32))
+            w4b[g] = t
 
         hs = keep.tile([P, NG, 4], F32, name="hs")
         w5 = keep.tile([P, NG, 1024], U8, name="w5", align_bytes=64)
@@ -96,24 +96,27 @@ def tile_additivecoupling_pa_w4_kernel(
         load_h3(0, 1, 2)
         nc.sync.dma_start(out=hs[:], in_=h3_scale.rearrange("o (g p t) -> p (o g) t", p=P, t=4))
         load_h3(0, 2, 4)
-        load_scales(w4s[0][:, 0:1, :], W4_scales[0:1, :, 0:1024])
-        load_w4_group(0)
+        load_scales(nc.sync, w4s[0][:, 0:2, :], W4_scales[0:2, :, 0:1024])
+        load_w4_groups(0, 1)
+        load_w4_groups(1, 2)
         load_h3(1, 0, 2)
-        load_scales(w4s[0][:, 1:4, :], W4_scales[1:4, :, 0:1024])
-        load_w4_group(1)
+        load_scales(nc.sync, w4s[0][:, 2:4, :], W4_scales[2:4, :, 0:1024])
+        load_w4_groups(2, 3)
         load_h3(1, 2, 4)
-        load_w4_group(2)
-        load_w4_group(3)
-        load_scales(w4s[1], W4_scales[:, :, 1024:2048])
-        load_w4_channels(2)
-        load_w4_channels(3)
+        load_w4_groups(3, 4)
+        load_scales(nc.sync, w4s[1][:, 0:2, :], W4_scales[0:2, :, 1024:2048])
+        load_w4_upper(0)
+        load_w4_upper(1)
+        load_scales(nc.sync, w4s[1][:, 2:4, :], W4_scales[2:4, :, 1024:2048])
+        load_w4_upper(2)
+        load_w4_upper(3)
         nc.sync.dma_start(out=xt[0][:], in_=xv[0])
         nc.sync.dma_start(out=b5bc[:], in_=b5.partition_broadcast(P))
 
         def load_late():
-            nc.sync.dma_start(out=xt[1][:], in_=xv[1])
-            load_scales(w5s, W5_scales)
+            load_scales(nc.sync, w5s, W5_scales)
             nc.sync.dma_start(out=w5[:].bitcast(I32), in_=W5_words.rearrange("g p n -> p g n").bitcast(I32))
+            nc.sync.dma_start(out=xt[1][:], in_=xv[1])
 
         wide, ordered, turned, scaled, h3q, h3s = {}, {}, {}, {}, {}, {}
         for h in range(2):
@@ -273,20 +276,30 @@ def tile_additivecoupling_pa_w4_kernel(
 
         summed, back, relud = {}, {}, {}
 
-        def token_tile(h, i, o, bank_name):
-            bank = psum.tile([P, 512], F32, name="acct", tag=bank_name)
+        def token_pass(h, i, o, g):
             cols = slice(P * i, P * (i + 1))
+            nc.tensor.matmul_mx(
+                out=summed[h, i, o][:],
+                lhsT=h3q[h, g][:, cols].bitcast(FP8X4),
+                lhsT_scale=h3s[h, g][:, cols],
+                rhs=w4b[g][:, 1024 * (o - 2) : 1024 * (o - 1)].bitcast(FP4X4),
+                rhs_scale=w4s[1][:, g, 512 * (o - 2) : 512 * (o - 1)],
+                start=(g == 0),
+                stop=(g == NG - 1),
+            )
+
+        def token_tile(h, i, o, bank_name):
+            summed[h, i, o] = psum.tile([P, 512], F32, name="acct", tag=bank_name)
             for g in range(NG):
-                nc.tensor.matmul_mx(
-                    out=bank[:],
-                    lhsT=h3q[h, g][:, cols].bitcast(FP8X4),
-                    lhsT_scale=h3s[h, g][:, cols],
-                    rhs=w4b[o][:, g, :].bitcast(FP4X4),
-                    rhs_scale=w4s[1][:, g, 512 * (o - 2) : 512 * (o - 1)],
-                    start=(g == 0),
-                    stop=(g == NG - 1),
-                )
-            summed[h, i, o] = bank
+                token_pass(h, i, o, g)
+
+        def token_sweep(h, bank_names):
+            units = [(i, o) for i in range(2) for o in (2, 3)]
+            for (i, o), name in zip(units, bank_names):
+                summed[h, i, o] = psum.tile([P, 512], F32, name="acct", tag=name)
+            for g in range(NG):
+                for i, o in units:
+                    token_pass(h, i, o, g)
 
         def add_b4(h, i, o):
             t = work.tile([P, 2, P, 2], BF16, name="biased", tag="biased", bufs=4, align_bytes=64)
@@ -374,16 +387,14 @@ def tile_additivecoupling_pa_w4_kernel(
         def add_m(h, i):
             nc.vector.tensor_tensor(out=pair[h, i][:, 0, :], in0=acc2[h, i][:], in1=pair[h, i][:, 0, :], op=ALU.add)
 
-        def lay_side_by_side(h, i):
-            t = keep.tile([P, HALF, 2], F32, name="xb")
-            nc.scalar.copy(out=t[:], in_=pair[h, i][:].rearrange("p r j -> p j r"))
-            return t
-
-        def finish_last(h, i, banks, xb):
+        def finish_last(h, i, banks):
             for n, bank in enumerate(banks):
                 t = keep.tile([P, 256, 2], F32, name=f"last{n}")
                 nc.vector.tensor_tensor(
-                    out=t[:], in0=bank[:].rearrange("p r j -> p j r"), in1=xb[:, 256 * n : 256 * (n + 1), :], op=ALU.add
+                    out=t[:],
+                    in0=bank[:].rearrange("p r j -> p j r"),
+                    in1=pair[h, i][:, :, 256 * n : 256 * (n + 1)].rearrange("p r j -> p j r"),
+                    op=ALU.add,
                 )
                 nc.sync.dma_start(out=outv[h, :, i, 512 * n : 512 * (n + 1)], in_=t[:].rearrange("p j r -> p (j r)"))
 
@@ -456,34 +467,26 @@ def tile_additivecoupling_pa_w4_kernel(
         for g in range(1, NG):
             scale(1, g)
             quantise_h3(1, g - 1)
-        token_tile(0, 0, 2, "b5")
-        token_tile(0, 1, 2, "b6")
-        token_tile(0, 0, 3, "b7")
-        token_tile(0, 1, 3, "b4")
-        add_b4(0, 0, 2)
         quantise_h3(1, NG - 1)
-        add_b4(0, 0, 3)
-        add_b4(0, 1, 2)
-        add_b4(0, 1, 3)
+        token_sweep(0, ("b5", "b6", "b0", "b7"))
+        for i in range(2):
+            for o in (2, 3):
+                add_b4(0, i, o)
         for i in range(2):
             x_odd(0, i)
-        interleave_on_scalar(0, 0)
-        x_odd(1, 1)
-        channel_tiles(1, 0, "b0")
+        channel_tiles(1, 0, "b1")
         relu_move(1, 0)
-        x_even(1, 1)
+        interleave_on_scalar(0, 0)
         interleave(0, 1)
         x_even(0, 0)
-        for g in range(2):
-            quantise_moved(0, g)
-        channel_tiles(1, 1, "b1")
-        turn_back(0, 0, (2, 3), "b2")
-        turn_back(0, 1, (2, 3), "b3")
-        x_odd(1, 0)
+        quantise_moved(0, 1)
+        quantise_moved(0, 0)
+        channel_tiles(1, 1, "b2")
+        turn_back(0, 0, (2, 3), "b3")
+        turn_back(0, 1, (2, 3), "b4")
         relu_move(1, 1)
         relu_back(0, 0, (2, 3))
         x_even(0, 1)
-        x_even(1, 0)
         quantise_back(0, 0, (2, 3))
         channel_tiles(1, 2, "b5")
         relu_move(1, 2)
@@ -493,17 +496,19 @@ def tile_additivecoupling_pa_w4_kernel(
         stage2(0, 0, "b7")
         token_tile(1, 0, 2, "b0")
         token_tile(1, 0, 3, "b2")
+        x_even(1, 0)
         add_m(0, 0)
-        xb = lay_side_by_side(1, 1)
         store(0, 0, HALF)
         quantise_back(0, 1, (2, 3))
-        stage2(0, 1, "b4")
+        stage2(0, 1, "b3")
         add_b4(1, 0, 2)
         add_b4(1, 0, 3)
+        x_odd(1, 0)
+        x_odd(1, 1)
         interleave_on_scalar(1, 0)
         interleave(1, 1)
         turn_back(1, 0, (2, 3), "b1")
-        token_tile(1, 1, 2, "b3")
+        token_tile(1, 1, 2, "b4")
         token_tile(1, 1, 3, "b6")
         add_m(0, 1)
         relu_back(1, 0, (2, 3))
@@ -516,12 +521,13 @@ def tile_additivecoupling_pa_w4_kernel(
         add_b4(1, 1, 3)
         stage2(1, 0, "b0")
         relu_back(1, 1, (2,))
-        turn_back(1, 1, (3,), "b4")
+        turn_back(1, 1, (3,), "b3")
         last = zero_banks(("b2", "b5"))
+        x_even(1, 1)
         quantise_back(1, 1, (2,))
         relu_back(1, 1, (3,))
         add_m(1, 0)
         quantise_back(1, 1, (3,))
         stage2_last(1, 1, last)
         store(1, 0, 256)
-        finish_last(1, 1, last, xb)
+        finish_last(1, 1, last)

@@ -47,8 +47,9 @@ def tile_additivecoupling_pa_w4_kernel(
         nc.vector.memset(ones[:], 1.0)
         nc.vector.memset(w4s[0][:].rearrange("p g n -> p (g n)").bitcast(I32), 0)
         nc.vector.tensor_copy(out=identb[:], in_=ident[:])
-        nc.vector.memset(w4s[1][:].rearrange("p g n -> p (g n)").bitcast(I32), 0)
-        nc.vector.memset(w5s[:].rearrange("p g n -> p (g n)").bitcast(I32), 0)
+
+        def clear(plane):
+            nc.vector.memset(plane.rearrange("p g n -> p (g n)").bitcast(I32), 0)
 
         hb = {}
 
@@ -104,14 +105,15 @@ def tile_additivecoupling_pa_w4_kernel(
         load_w4_groups(2, 3)
         load_h3(1, 2, 4)
         load_w4_groups(3, 4)
-        load_scales(nc.sync, w4s[1][:, 0:2, :], W4_scales[0:2, :, 1024:2048])
-        load_w4_upper(0)
-        load_w4_upper(1)
-        load_scales(nc.sync, w4s[1][:, 2:4, :], W4_scales[2:4, :, 1024:2048])
-        load_w4_upper(2)
-        load_w4_upper(3)
-        nc.sync.dma_start(out=xt[0][:], in_=xv[0])
-        nc.sync.dma_start(out=b5bc[:], in_=b5.partition_broadcast(P))
+
+        def load_upper(g0):
+            load_scales(nc.sync, w4s[1][:, g0 : g0 + 2, :], W4_scales[g0 : g0 + 2, :, 1024:2048])
+            load_w4_upper(g0)
+            load_w4_upper(g0 + 1)
+
+        def load_x0():
+            nc.sync.dma_start(out=xt[0][:], in_=xv[0])
+            nc.sync.dma_start(out=b5bc[:], in_=b5.partition_broadcast(P))
 
         def load_late():
             load_scales(nc.sync, w5s, W5_scales)
@@ -400,11 +402,13 @@ def tile_additivecoupling_pa_w4_kernel(
 
         def store(h, i, split):
             t = keep.tile([P, HALF, 2], F32, name=f"o{h}{i}")
-            parts = [(nc.vector.tensor_copy, split, HALF), (nc.scalar.copy, 0, split)]
+            parts = [(nc.scalar.copy, 0, split), (nc.vector.tensor_copy, split, HALF)]
             for copy, lo, hi in parts:
                 if lo < hi:
                     copy(out=t[:, lo:hi, :], in_=pair[h, i][:, :, lo:hi].rearrange("p r j -> p j r"))
-            nc.sync.dma_start(out=outv[h, :, i, :], in_=t[:].rearrange("p j r -> p (j r)"))
+                    nc.sync.dma_start(
+                        out=outv[h, :, i, 2 * lo : 2 * hi], in_=t[:, lo:hi, :].rearrange("p j r -> p (j r)")
+                    )
 
         def sweep_passes(g):
             for q in range(4):
@@ -446,20 +450,24 @@ def tile_additivecoupling_pa_w4_kernel(
         sweep_passes(0)
         turn(0, 3, (0, 1), "b4")
         scale(0, 1)
-        scale_tile(0, 2, 0)
+        clear(w4s[1][:, 0:2, :])
+        load_upper(0)
         quantise_h3(0, 1)
         sweep_passes(1)
         turn(1, 0, (0, 1), "b5")
         turn(1, 1, (0, 1), "b6")
-        scale_tile(0, 2, 1)
-        scale_tile(0, 3, 0)
+        scale(0, 2)
+        clear(w4s[1][:, 2:4, :])
+        load_upper(2)
+        load_x0()
         quantise_h3(0, 2)
         sweep_passes(2)
         turn(1, 2, (0, 1), "b7")
-        scale_tile(0, 3, 1)
+        scale(0, 3)
+        clear(w5s[:])
+        quantise_h3(0, 3)
         turn(1, 3, (0, 1), "b4")
         scale(1, 0)
-        quantise_h3(0, 3)
         sweep_passes(3)
         for q in range(4):
             relu_move(0, q)
@@ -468,21 +476,21 @@ def tile_additivecoupling_pa_w4_kernel(
             scale(1, g)
             quantise_h3(1, g - 1)
         quantise_h3(1, NG - 1)
-        token_sweep(0, ("b5", "b6", "b0", "b7"))
+        token_sweep(0, ("b5", "b0", "b1", "b6"))
         for i in range(2):
             for o in (2, 3):
                 add_b4(0, i, o)
         for i in range(2):
             x_odd(0, i)
-        channel_tiles(1, 0, "b1")
+        channel_tiles(1, 0, "b2")
         relu_move(1, 0)
         interleave_on_scalar(0, 0)
         interleave(0, 1)
         x_even(0, 0)
         quantise_moved(0, 1)
         quantise_moved(0, 0)
-        channel_tiles(1, 1, "b2")
-        turn_back(0, 0, (2, 3), "b3")
+        channel_tiles(1, 1, "b3")
+        turn_back(0, 0, (2, 3), "b7")
         turn_back(0, 1, (2, 3), "b4")
         relu_move(1, 1)
         relu_back(0, 0, (2, 3))
@@ -493,10 +501,11 @@ def tile_additivecoupling_pa_w4_kernel(
         channel_tiles(1, 3, "b6")
         relu_move(1, 3)
         relu_back(0, 1, (2, 3))
-        stage2(0, 0, "b7")
+        stage2(0, 0, "b1")
         token_tile(1, 0, 2, "b0")
         token_tile(1, 0, 3, "b2")
         x_even(1, 0)
+        x_even(1, 1)
         add_m(0, 0)
         store(0, 0, HALF)
         quantise_back(0, 1, (2, 3))
@@ -507,7 +516,7 @@ def tile_additivecoupling_pa_w4_kernel(
         x_odd(1, 1)
         interleave_on_scalar(1, 0)
         interleave(1, 1)
-        turn_back(1, 0, (2, 3), "b1")
+        turn_back(1, 0, (2, 3), "b7")
         token_tile(1, 1, 2, "b4")
         token_tile(1, 1, 3, "b6")
         add_m(0, 1)
@@ -517,16 +526,15 @@ def tile_additivecoupling_pa_w4_kernel(
         quantise_moved(1, 0)
         add_b4(1, 1, 2)
         quantise_back(1, 0, (2, 3))
-        turn_back(1, 1, (2,), "b7")
+        turn_back(1, 1, (2,), "b1")
         add_b4(1, 1, 3)
         stage2(1, 0, "b0")
         relu_back(1, 1, (2,))
         turn_back(1, 1, (3,), "b3")
         last = zero_banks(("b2", "b5"))
-        x_even(1, 1)
+        add_m(1, 0)
         quantise_back(1, 1, (2,))
         relu_back(1, 1, (3,))
-        add_m(1, 0)
         quantise_back(1, 1, (3,))
         stage2_last(1, 1, last)
         store(1, 0, 256)

@@ -32,24 +32,25 @@ def tile_additivecoupling_pa_w4_kernel(
         ctx.enter_context(tc.manual_schedule())
 
         rows = keep.tile([P, P], BF16, name="rows")
-        nc.gpsimd.memset(rows[:], 0.0)
         ident = keep.tile([P, P], F32, name="ident")
-        make_identity(nc, ident[:])
+        identb = keep.tile([P, P], BF16, name="identb")
+        zeros = keep.tile([P, 512], BF16, name="zeros")
+        ones = keep.tile([P, 1], F32, name="ones")
         w4s = []
         for part in range(2):
             s_p = keep.tile([P, NG, 1024], U8, name=f"w4s{part}", align_bytes=64)
             w4s.append(s_p)
         w5s = keep.tile([P, NG, HALF], U8, name="w5s", align_bytes=64)
-        zeros = keep.tile([P, 512], BF16, name="zeros")
-        identb = keep.tile([P, P], BF16, name="identb")
-        ones = keep.tile([P, 1], F32, name="ones")
-        nc.vector.memset(zeros[:], 0.0)
-        nc.vector.memset(ones[:], 1.0)
-        nc.vector.memset(w4s[0][:].rearrange("p g n -> p (g n)").bitcast(I32), 0)
-        nc.vector.tensor_copy(out=identb[:], in_=ident[:])
 
         def clear(plane):
             nc.vector.memset(plane.rearrange("p g n -> p (g n)").bitcast(I32), 0)
+
+        nc.vector.memset(zeros[:], 0.0)
+        nc.vector.memset(rows[:], 0.0)
+        clear(w4s[0][:])
+        nc.vector.memset(ones[:], 1.0)
+        nc.vector.memset(ident[:], 0.0)
+        make_identity(nc, ident[:], nomemset=True)
 
         hb = {}
 
@@ -420,24 +421,25 @@ def tile_additivecoupling_pa_w4_kernel(
             for n in range(count):
                 nc.tensor.matmul(out=bank[:], lhsT=zeros[:, 0:P], rhs=zeros[:], start=True, stop=True)
 
-        warm_up(3)
-        spread = [spread_b4(o, f"b{o - 1}") for o in (2, 3)]
-        for g in range(2):
-            for i in range(2):
-                widen_sorted(0, g, i)
-        keep_b4_row(2, spread[0], by_activation)
-        keep_b4_row(3, spread[1], nc.scalar.copy)
+        warm_up(5)
+        widen_sorted(0, 0, 0)
+        widen_sorted(0, 0, 1)
+        nc.vector.tensor_copy(out=identb[:], in_=ident[:])
+        widen_sorted(0, 1, 0)
+        widen_sorted(0, 1, 1)
         turn(0, 0, (0,), "b4")
         turn(0, 0, (1,), "b5")
-        columns = turn_b4("b3")
+        columns = turn_b4("b1")
         turn(0, 1, (0, 1), "b6")
-        warm_up(2)
-        for i in range(2):
-            widen(0, 2, i, nc.scalar.copy)
+        spread = [spread_b4(o, f"b{o}") for o in (2, 3)]
+        widen(0, 2, 0, by_activation)
+        widen(0, 2, 1, nc.scalar.copy)
         nc.scalar.copy(out=b4c[:], in_=columns[:, 0:8])
         turn(0, 2, (0, 1), "b7")
-        for i in range(2):
-            widen(0, 3, i, nc.scalar.copy)
+        widen(0, 3, 0, nc.scalar.copy)
+        for o in (2, 3):
+            keep_b4_row(o, spread[o - 2], nc.scalar.copy)
+        widen(0, 3, 1, nc.scalar.copy)
         for g in range(NG):
             for i in range(2):
                 widen(1, g, i, nc.scalar.copy)

@@ -95,6 +95,7 @@ def tile_additivecoupling_pa_w4_kernel(
 
         load_h3(0, 0, 1)
         nc.scalar.dma_start(out=rows[0:16, :], in_=b4.rearrange("(c n) -> c n", c=16))
+        nc.scalar.dma_start(out=rows[32:36, :], in_=b5.rearrange("(c n) -> c n", c=4))
         load_h3(0, 1, 2)
         nc.sync.dma_start(out=hs[:], in_=h3_scale.rearrange("o (g p t) -> p (o g) t", p=P, t=4))
         load_h3(0, 2, 4)
@@ -114,7 +115,6 @@ def tile_additivecoupling_pa_w4_kernel(
 
         def load_x0():
             nc.sync.dma_start(out=xt[0][:], in_=xv[0])
-            nc.sync.dma_start(out=b5bc[:], in_=b5.partition_broadcast(P))
 
         def load_late():
             load_scales(nc.sync, w5s, W5_scales)
@@ -166,9 +166,28 @@ def tile_additivecoupling_pa_w4_kernel(
                 op=ALU.mult,
             )
 
+        product = {}
+
+        def multiply(h, g):
+            t = work.tile([P, 2, NT, 2], BF16, name="product", tag="product", bufs=4, align_bytes=64)
+            words = turned[h, g][:].rearrange("p u i m -> p u (i m)")
+            nc.vector.tensor_tensor(
+                out=t[:],
+                in0=words.bitcast(BF16).rearrange("p u (c e) -> p u c e", e=2),
+                in1=hs[:, g, :].rearrange("p (u e) -> p u e", u=2).unsqueeze(2).to_broadcast([P, 2, NT, 2]),
+                op=ALU.mult,
+            )
+            product[h, g] = t
+
+        def join(h, g):
+            nc.scalar.copy(
+                out=scaled_tile(h, g)[:].rearrange("p c t -> p (c t)").bitcast(F32).rearrange("p (c u) -> p c u", u=2),
+                in_=product[h, g][:].rearrange("p u c e -> p (u c e)").bitcast(F32).rearrange("p (u c) -> p c u", u=2),
+            )
+
         def scaled_tile(h, g):
             if (h, g) not in scaled:
-                t = work.tile([P, NT, 4], BF16, name="scaled", tag="scaled", bufs=3, align_bytes=64)
+                t = work.tile([P, NT, 4], BF16, name="scaled", tag="scaled", bufs=4, align_bytes=64)
                 scaled[h, g] = t
             return scaled[h, g]
 
@@ -203,10 +222,10 @@ def tile_additivecoupling_pa_w4_kernel(
             nc.tensor.transpose(bank[:], rows[:], identb[:])
             return bank
 
-        def spread_b4(o, bank_name):
+        def spread_rows(r0, bank_name):
             bank = psum.tile([P, 4, P], F32, name="rowbank", tag=bank_name)
             for n in range(4):
-                r = 4 * o + n
+                r = r0 + n
                 nc.tensor.matmul(
                     out=bank[:, n, :], lhsT=identb[:, r : r + 1].to_broadcast([P, P]), rhs=rows[:], start=True, stop=True
                 )
@@ -300,9 +319,11 @@ def tile_additivecoupling_pa_w4_kernel(
             units = [(i, o) for i in range(2) for o in (2, 3)]
             for (i, o), name in zip(units, bank_names):
                 summed[h, i, o] = psum.tile([P, 512], F32, name="acct", tag=name)
-            for g in range(NG):
-                for i, o in units:
-                    token_pass(h, i, o, g)
+            for g0 in (0, 2):
+                for i in range(2):
+                    for g in (g0, g0 + 1):
+                        for o in (2, 3):
+                            token_pass(h, i, o, g)
 
         def add_b4(h, i, o):
             t = work.tile([P, 2, P, 2], BF16, name="biased", tag="biased", bufs=4, align_bytes=64)
@@ -431,7 +452,7 @@ def tile_additivecoupling_pa_w4_kernel(
         turn(0, 0, (1,), "b5")
         columns = turn_b4("b1")
         turn(0, 1, (0, 1), "b6")
-        spread = [spread_b4(o, f"b{o}") for o in (2, 3)]
+        spread = [spread_rows(4 * o, f"b{o}") for o in (2, 3)]
         widen(0, 2, 0, by_activation)
         widen(0, 2, 1, nc.scalar.copy)
         nc.scalar.copy(out=b4c[:], in_=columns[:, 0:8])
@@ -469,21 +490,25 @@ def tile_additivecoupling_pa_w4_kernel(
         clear(w5s[:])
         quantise_h3(0, 3)
         turn(1, 3, (0, 1), "b4")
-        scale(1, 0)
+        for g in range(NG):
+            multiply(1, g)
+        join(1, 0)
         sweep_passes(3)
         for q in range(4):
             relu_move(0, q)
+            if q > 0:
+                join(1, q)
         load_late()
-        for g in range(1, NG):
-            scale(1, g)
-            quantise_h3(1, g - 1)
-        quantise_h3(1, NG - 1)
-        token_sweep(0, ("b5", "b0", "b1", "b6"))
+        for g in range(NG):
+            quantise_h3(1, g)
+        token_sweep(0, ("b5", "b6", "b0", "b1"))
+        b5_rows = spread_rows(32, "b7")
         for i in range(2):
             for o in (2, 3):
                 add_b4(0, i, o)
         for i in range(2):
             x_odd(0, i)
+        nc.scalar.copy(out=b5bc[:], in_=b5_rows[:].rearrange("m n c -> m (n c)"))
         channel_tiles(1, 0, "b2")
         relu_move(1, 0)
         interleave_on_scalar(0, 0)

from contextlib import ExitStack

import concourse.mybir as mybir
from concourse.masks import make_identity

B, HALF, MID = 512, 512, 2048
FLOPS = 2 * B * MID * MID + 2 * B * MID * HALF

P = 128
NG = MID // 512
NT = 256
F32 = mybir.dt.float32
BF16 = mybir.dt.bfloat16
U8 = mybir.dt.uint8
U32 = mybir.dt.uint32
I32 = mybir.dt.int32
FP8 = mybir.dt.float8_e4m3fn
FP8X4 = mybir.dt.float8_e4m3fn_x4
FP4X4 = mybir.dt.float4_e2m1fn_x4
ALU = mybir.AluOpType
ACT = mybir.ActivationFunctionType


def tile_additivecoupling_pa_w4_kernel(
    tc, x, h3_bytes, h3_scale, W4_words, W4_scales, b4, W5_words, W5_scales, b5, out
):
    nc = tc.nc
    with ExitStack() as ctx:
        keep = ctx.enter_context(tc.tile_pool(name="keep", bufs=1))
        work = ctx.enter_context(tc.tile_pool(name="work", bufs=2))
        psum = ctx.enter_context(tc.psum_pool(name="psum", bufs=1))
        ctx.enter_context(tc.manual_schedule())

        rows = keep.tile([P, P], BF16, name="rows")
        ident = keep.tile([P, P], F32, name="ident")
        identb = keep.tile([P, P], BF16, name="identb")
        zeros = keep.tile([P, 512], BF16, name="zeros")
        ones = keep.tile([P, 1], F32, name="ones")
        w4s = []
        for part in range(2):
            s_p = keep.tile([P, NG, 1024], U8, name=f"w4s{part}", align_bytes=64)
            w4s.append(s_p)
        w5s = keep.tile([P, NG, HALF], U8, name="w5s", align_bytes=64)

        def clear(plane):
            nc.vector.memset(plane.rearrange("p g n -> p (g n)").bitcast(I32), 0)

        nc.vector.memset(zeros[:], 0.0)
        nc.vector.memset(rows[:], 0.0)
        clear(w4s[0][:])
        nc.vector.memset(ones[:], 1.0)
        nc.vector.memset(ident[:], 0.0)
        make_identity(nc, ident[:], nomemset=True)

        hb = {}

        def load_h3(h, g0, g1):
            t = keep.tile([P, 2, 512 * (g1 - g0)], U8, name=f"hb{h}_{g0}", align_bytes=64)
            src = h3_bytes.rearrange("(h p i) k -> h p i k", h=2, i=2)
            nc.sync.dma_start(out=t[:], in_=src[h, :, :, 512 * g0 : 512 * g1])
            for g in range(g0, g1):
                hb[h, g] = t[:, :, 512 * (g - g0) : 512 * (g - g0 + 1)]

        def load_scales(queue, dst, src):
            for r in range(4):
                queue.dma_start(
                    out=dst[r:P:32, :, :].bitcast(I32), in_=src[:, r:16:4, :].rearrange("g q n -> q g n").bitcast(I32)
                )

        w4 = {}

        def load_w4_groups(g0, g1):
            t = keep.tile([P, g1 - g0, 2048], U8, name=f"w4a{g0}", align_bytes=64)
            nc.sync.dma_start(
                out=t[:].bitcast(I32), in_=W4_words[g0:g1, :, 0:2048].rearrange("g p n -> p g n").bitcast(I32)
            )
            for g in range(g0, g1):
                w4[g] = t[:, g - g0, :]

        w4b = {}

        def load_w4_upper(g):
            t = keep.tile([P, 2048], U8, name=f"w4b{g}", align_bytes=64)
            nc.sync.dma_start(out=t[:].bitcast(I32), in_=W4_words[g, :, 2048:4096].bitcast(I32))
            w4b[g] = t

        hs = keep.tile([P, NG, 4], F32, name="hs")
        w5 = keep.tile([P, NG, 1024], U8, name="w5", align_bytes=64)
        b5bc = keep.tile([P, HALF], BF16, name="b5bc")
        xv = x.rearrange("(h p i) c -> h p i c", h=2, i=2)
        xt = []
        for h in range(2):
            x_h = keep.tile([P, 2, 2 * HALF], BF16, name=f"xt{h}")
            xt.append(x_h)

        load_h3(0, 0, 1)
        nc.scalar.dma_start(out=rows[0:16, :], in_=b4.rearrange("(c n) -> c n", c=16))
        nc.scalar.dma_start(out=rows[32:36, :], in_=b5.rearrange("(c n) -> c n", c=4))
        load_h3(0, 1, 2)
        nc.sync.dma_start(out=hs[:], in_=h3_scale.rearrange("o (g p t) -> p (o g) t", p=P, t=4))
        load_h3(0, 2, 4)
        load_scales(nc.sync, w4s[0][:, 0:2, :], W4_scales[0:2, :, 0:1024])
        load_w4_groups(0, 1)
        load_w4_groups(1, 2)
        load_h3(1, 0, 2)
        load_scales(nc.sync, w4s[0][:, 2:4, :], W4_scales[2:4, :, 0:1024])
        load_w4_groups(2, 3)
        load_h3(1, 2, 4)
        load_w4_groups(3, 4)

        def load_upper(g0):
            load_scales(nc.sync, w4s[1][:, g0 : g0 + 2, :], W4_scales[g0 : g0 + 2, :, 1024:2048])
            load_w4_upper(g0)
            load_w4_upper(g0 + 1)

        def load_x0():
            nc.sync.dma_start(out=xt[0][:], in_=xv[0])

        def load_late():
            load_scales(nc.sync, w5s, W5_scales)
            nc.sync.dma_start(out=w5[:].bitcast(I32), in_=W5_words.rearrange("g p n -> p g n").bitcast(I32))
            nc.sync.dma_start(out=xt[1][:], in_=xv[1])

        wide, ordered, turned, scaled, h3q, h3s = {}, {}, {}, {}, {}, {}
        for h in range(2):
            for g in range(NG):
                h3q[h, g] = keep.tile([P, NT], U32, name=f"h3q{h}{g}", align_bytes=64)
                h3s[h, g] = keep.tile([P, NT], U8, name=f"h3s{h}{g}", align_bytes=64)

        def by_activation(out, in_):
            nc.scalar.activation(out=out, in_=in_, func=ACT.Copy)

        def widen(h, g, i, copy):
            t = work.tile([P, 512], BF16, name="wide", tag="wide", bufs=16, align_bytes=64)
            copy(out=t[:], in_=hb[h, g][:, i, :].bitcast(FP8))
            wide[h, g, i] = t

        def widen_sorted(h, g, i):
            t = work.tile([P, 2, P], F32, name="ordered", tag="ordered", bufs=8, align_bytes=64)
            nc.vector.tensor_scalar(
                out=t[:].rearrange("m u p -> m (u p)").bitcast(BF16).rearrange("m (u p e) -> m p u e", u=2, e=2),
                in0=hb[h, g][:, i, :].bitcast(FP8).rearrange("m (p u e) -> m p u e", u=2, e=2),
                scalar1=ones[:],
                scalar2=None,
                op0=ALU.mult,
            )
            ordered[h, g, i] = t

        def turn(h, g, tiles, bank_name):
            bank = psum.tile([P, 2, len(tiles), P], F32, name="turned", tag=bank_name)
            for n, i in enumerate(tiles):
                for u in range(2):
                    if (h, g, i) in ordered:
                        words = ordered[h, g, i][:, u, :]
                    else:
                        words = wide[h, g, i][:].bitcast(F32)[:, u::2]
                    nc.tensor.transpose(bank[:, u, n, :], words, ident[:])
                turned[h, g, i] = bank[:, :, n, :]
            turned[h, g] = bank

        def scale_into(dst, words, g, width):
            nc.vector.tensor_tensor(
                out=dst.rearrange("p c (u e) -> p c u e", u=2),
                in0=words.bitcast(BF16).rearrange("p u (c e) -> p c u e", e=2),
                in1=hs[:, g, :].rearrange("p (u e) -> p u e", u=2).unsqueeze(1).to_broadcast([P, width, 2, 2]),
                op=ALU.mult,
            )

        product = {}

        def multiply(h, g):
            t = work.tile([P, 2, NT, 2], BF16, name="product", tag="product", bufs=4, align_bytes=64)
            words = turned[h, g][:].rearrange("p u i m -> p u (i m)")
            nc.vector.tensor_tensor(
                out=t[:],
                in0=words.bitcast(BF16).rearrange("p u (c e) -> p u c e", e=2),
                in1=hs[:, g, :].rearrange("p (u e) -> p u e", u=2).unsqueeze(2).to_broadcast([P, 2, NT, 2]),
                op=ALU.mult,
            )
            product[h, g] = t

        def join(h, g):
            nc.scalar.copy(
                out=scaled_tile(h, g)[:].rearrange("p c t -> p (c t)").bitcast(F32).rearrange("p (c u) -> p c u", u=2),
                in_=product[h, g][:].rearrange("p u c e -> p (u c e)").bitcast(F32).rearrange("p (u c) -> p c u", u=2),
            )

        def scaled_tile(h, g):
            if (h, g) not in scaled:
                t = work.tile([P, NT, 4], BF16, name="scaled", tag="scaled", bufs=4, align_bytes=64)
                scaled[h, g] = t
            return scaled[h, g]

        def scale(h, g):
            scale_into(scaled_tile(h, g)[:], turned[h, g][:].rearrange("p u i m -> p u (i m)"), g, NT)

        def scale_tile(h, g, i):
            scale_into(scaled_tile(h, g)[:, P * i : P * (i + 1), :], turned[h, g, i], g, P)

        def quantise_into(src, codes, plane):
            nc.vector.quantize_mx(out=codes.bitcast(FP8X4), scales=plane, in_=src.rearrange("p c t -> p (c t)"))

        def quantise(src, name):
            width = src.shape[1]
            codes = keep.tile([P, width], U32, name=name + "q", align_bytes=64)
            plane = keep.tile([P, width], U8, name=name + "s", align_bytes=64)
            quantise_into(src[:], codes[:], plane[:])
            return codes, plane

        def quantise_h3(h, g):
            quantise_into(scaled[h, g][:], h3q[h, g][:], h3s[h, g][:])

        def quantise_h3_tile(h, g, i):
            cols = slice(P * i, P * (i + 1))
            quantise_into(scaled[h, g][:, cols, :], h3q[h, g][:, cols], h3s[h, g][:, cols])

        b4c = keep.tile([P, 8], F32, name="b4c")
        b4bc = keep.tile([P, 2, 512], BF16, name="b4bc")

        def turn_b4(bank_name):
            bank = psum.tile([P, P], BF16, name="b4bank", tag=bank_name)
            nc.tensor.transpose(bank[:], rows[:], identb[:])
            return bank

        def spread_rows(r0, bank_name):
            bank = psum.tile([P, 4, P], F32, name="rowbank", tag=bank_name)
            for n in range(4):
                r = r0 + n
                nc.tensor.matmul(
                    out=bank[:, n, :], lhsT=identb[:, r : r + 1].to_broadcast([P, P]), rhs=rows[:], start=True, stop=True
                )
            return bank

        def keep_b4_row(o, bank, copy):
            copy(
                out=b4bc[:, o - 2, :].rearrange("m (u p e) -> m u p e", u=2, e=2),
                in_=bank[:].rearrange("m n c -> m (n c)").rearrange("m (p u e) -> m u p e", u=2, e=2),
            )

        def pass1(dst, h, c, g, start, stop):
            nc.tensor.matmul_mx(
                out=dst,
                lhsT=w4[g][:, 256 * c : 256 * (c + 1)].bitcast(FP4X4),
                lhsT_scale=w4s[0][:, g, P * c : P * (c + 1)],
                rhs=h3q[h, g][:].bitcast(FP8X4),
                rhs_scale=h3s[h, g][:],
                start=start,
                stop=stop,
            )

        planes = {}

        def relu_and_move(h, bank, q):
            st = work.tile([P, 2, NT], BF16, name="staged", tag="staged", bufs=8, align_bytes=64)
            for j in range(2):
                c = 4 * j + q
                nc.scalar.activation(out=st[:, j, :], in_=bank[:, j, :], func=ACT.Relu, bias=b4c[:, c : c + 1])
            if h not in planes:
                t = keep.tile([P, 4, 2, NT], BF16, name=f"planes{h}", align_bytes=64)
                planes[h] = t
            nc.sync.dma_start(
                out=planes[h][32 * q : 32 * (q + 1)].rearrange("a t j c -> a (t j c)"),
                in_=st[:].rearrange("p j c -> p (j c)"),
            )

        summed_c = {}

        def channel_tiles(h, q, bank_name):
            bank = psum.tile([P, 2, NT], F32, name="acc", tag=bank_name)
            for j in range(2):
                for g in range(NG):
                    pass1(bank[:, j, :], h, 4 * j + q, g, g == 0, g == NG - 1)
            summed_c[h, q] = bank

        def relu_move(h, q):
            relu_and_move(h, summed_c[h, q], q)

        inter, h4q, h4s = {}, {}, {}

        def interleave_on_scalar(h, g):
            t = work.tile([P, NT, 4], BF16, name="inter", tag="inter", bufs=2, align_bytes=64)
            nc.scalar.copy(out=t[:], in_=planes[h][:, :, g, :].rearrange("p t c -> p c t"))
            inter[h, g] = t

        def interleave(h, g):
            t = work.tile([P, NT, 4], BF16, name="inter", tag="inter", bufs=2, align_bytes=64)
            nc.vector.tensor_copy(
                out=t[:].rearrange("p (c i) t -> p c t i", i=4),
                in_=planes[h][:, :, g, :].rearrange("p t (c i) -> p c t i", i=4),
            )
            inter[h, g] = t

        def quantise_moved(h, g):
            codes, plane = quantise(inter[h, g], f"h4_{h}{g}")
            for i in range(2):
                h4q[h, i, g] = codes[:, P * i : P * (i + 1)]
                h4s[h, i, g] = plane[:, P * i : P * (i + 1)]

        summed, back, relud = {}, {}, {}

        def token_pass(h, i, o, g):
            cols = slice(P * i, P * (i + 1))
            nc.tensor.matmul_mx(
                out=summed[h, i, o][:],
                lhsT=h3q[h, g][:, cols].bitcast(FP8X4),
                lhsT_scale=h3s[h, g][:, cols],
                rhs=w4b[g][:, 1024 * (o - 2) : 1024 * (o - 1)].bitcast(FP4X4),
                rhs_scale=w4s[1][:, g, 512 * (o - 2) : 512 * (o - 1)],
                start=(g == 0),
                stop=(g == NG - 1),
            )

        def token_tile(h, i, o, bank_name):
            summed[h, i, o] = psum.tile([P, 512], F32, name="acct", tag=bank_name)
            for g in range(NG):
                token_pass(h, i, o, g)

        def token_sweep(h, bank_names):
            units = [(i, o) for i in range(2) for o in (2, 3)]
            for (i, o), name in zip(units, bank_names):
                summed[h, i, o] = psum.tile([P, 512], F32, name="acct", tag=name)
            for g0 in (0, 2):
                for i in range(2):
                    for g in (g0, g0 + 1):
                        for o in (2, 3):
                            token_pass(h, i, o, g)

        def add_b4(h, i, o):
            t = work.tile([P, 2, P, 2], BF16, name="biased", tag="biased", bufs=4, align_bytes=64)
            nc.vector.tensor_tensor(
                out=t[:],
                in0=summed[h, i, o][:].rearrange("m (p u e) -> m u p e", u=2, e=2),
                in1=b4bc[:, o - 2, :].rearrange("m (u p e) -> m u p e", u=2, e=2),
                op=ALU.add,
            )
            summed[h, i, o] = t

        def turn_back(h, i, groups, bank_name):
            bank = psum.tile([P, 2, len(groups), P], F32, name="back", tag=bank_name)
            for n, o in enumerate(groups):
                words = summed[h, i, o][:].rearrange("m u p e -> m (u p e)").bitcast(F32)
                for u in range(2):
                    nc.tensor.transpose(bank[:, u, n, :], words[:, P * u : P * (u + 1)], ident[:])
            back[h, i, groups] = bank

        def relu_back(h, i, groups):
            t = work.tile([P, len(groups) * P, 4], BF16, name="relud", tag="relud", bufs=4, align_bytes=64)
            halves = back[h, i, groups][:].rearrange("p u o m -> p (u o m)").bitcast(BF16)
            nc.scalar.activation(
                out=t[:].rearrange("p c (u e) -> p c u e", u=2),
                in_=halves.rearrange("p (u c e) -> p c u e", u=2, e=2),
                func=ACT.Relu,
            )
            relud[h, i, groups] = t

        def quantise_back(h, i, groups):
            codes, plane = quantise(relud[h, i, groups], f"h4_{h}{i}_{groups[0]}")
            for n, g in enumerate(groups):
                h4q[h, i, g] = codes[:, P * n : P * (n + 1)]
                h4s[h, i, g] = plane[:, P * n : P * (n + 1)]

        acc2, pair = {}, {}

        def stage2(h, i, bank_name):
            bank = psum.tile([P, HALF], F32, name="acc2", tag=bank_name)
            acc2[h, i] = bank
            for g in range(NG):
                nc.tensor.matmul_mx(
                    out=bank[:],
                    lhsT=h4q[h, i, g].bitcast(FP8X4),
                    lhsT_scale=h4s[h, i, g],
                    rhs=w5[:, g, :].bitcast(FP4X4),
                    rhs_scale=w5s[:, g, :],
                    start=(g == 0),
                    stop=(g == NG - 1),
                )

        def zero_banks(bank_names):
            banks = []
            for name in bank_names:
                bank = psum.tile([P, 2, 256], F32, name="acc2z", tag=name)
                nc.tensor.matmul(out=bank[:, 1, :], lhsT=zeros[:, 0:P], rhs=zeros[:, 0:256], start=True, stop=True)
                banks.append(bank)
            return banks

        def stage2_last(h, i, banks):
            for g in range(NG):
                for n, bank in enumerate(banks):
                    nc.tensor.matmul_mx(
                        out=bank[:, 0, :],
                        lhsT=h4q[h, i, g].bitcast(FP8X4),
                        lhsT_scale=h4s[h, i, g],
                        rhs=w5[:, g, 512 * n : 512 * (n + 1)].bitcast(FP4X4),
                        rhs_scale=w5s[:, g, 256 * n : 256 * (n + 1)],
                        start=(g == 0),
                        stop=(g == NG - 1),
                    )

        for h in range(2):
            for i in range(2):
                pair[h, i] = keep.tile([P, 2, HALF], F32, name=f"pair{h}{i}")

        def x_odd(h, i):
            nc.scalar.copy(out=pair[h, i][:, 1, :], in_=xt[h][:, i, 1::2])

        def x_even(h, i):
            nc.vector.tensor_tensor(out=pair[h, i][:, 0, :], in0=xt[h][:, i, 0::2], in1=b5bc[:], op=ALU.add)

        outv = out.rearrange("(h p i) c -> h p i c", h=2, i=2)

        def add_m(h, i):
            nc.vector.tensor_tensor(out=pair[h, i][:, 0, :], in0=acc2[h, i][:], in1=pair[h, i][:, 0, :], op=ALU.add)

        def finish_last(h, i, banks):
            for n, bank in enumerate(banks):
                t = keep.tile([P, 256, 2], F32, name=f"last{n}")
                nc.vector.tensor_tensor(
                    out=t[:],
                    in0=bank[:].rearrange("p r j -> p j r"),
                    in1=pair[h, i][:, :, 256 * n : 256 * (n + 1)].rearrange("p r j -> p j r"),
                    op=ALU.add,
                )
                nc.sync.dma_start(out=outv[h, :, i, 512 * n : 512 * (n + 1)], in_=t[:].rearrange("p j r -> p (j r)"))

        def store(h, i, split):
            t = keep.tile([P, HALF, 2], F32, name=f"o{h}{i}")
            parts = [(nc.scalar.copy, 0, split), (nc.vector.tensor_copy, split, HALF)]
            for copy, lo, hi in parts:
                if lo < hi:
                    copy(out=t[:, lo:hi, :], in_=pair[h, i][:, :, lo:hi].rearrange("p r j -> p j r"))
                    nc.sync.dma_start(
                        out=outv[h, :, i, 2 * lo : 2 * hi], in_=t[:, lo:hi, :].rearrange("p j r -> p (j r)")
                    )

        def sweep_passes(g):
            for q in range(4):
                for j in range(2):
                    pass1(summed_c[0, q][:, j, :], 0, 4 * j + q, g, g == 0 and j == 0, g == NG - 1 and j == 1)

        def warm_up(count):
            bank = psum.tile([P, 512], F32, name="unread", tag="b0")
            for n in range(count):
                nc.tensor.matmul(out=bank[:], lhsT=zeros[:, 0:P], rhs=zeros[:], start=True, stop=True)

        warm_up(5)
        widen_sorted(0, 0, 0)
        widen_sorted(0, 0, 1)
        nc.vector.tensor_copy(out=identb[:], in_=ident[:])
        widen_sorted(0, 1, 0)
        widen_sorted(0, 1, 1)
        turn(0, 0, (0,), "b4")
        turn(0, 0, (1,), "b5")
        columns = turn_b4("b1")
        turn(0, 1, (0, 1), "b6")
        spread = [spread_rows(4 * o, f"b{o}") for o in (2, 3)]
        widen(0, 2, 0, by_activation)
        widen(0, 2, 1, nc.scalar.copy)
        nc.scalar.copy(out=b4c[:], in_=columns[:, 0:8])
        turn(0, 2, (0, 1), "b7")
        widen(0, 3, 0, nc.scalar.copy)
        for o in (2, 3):
            keep_b4_row(o, spread[o - 2], nc.scalar.copy)
        widen(0, 3, 1, nc.scalar.copy)
        for g in range(NG):
            for i in range(2):
                widen(1, g, i, nc.scalar.copy)
        for q in range(4):
            summed_c[0, q] = psum.tile([P, 2, NT], F32, name="acc", tag=f"b{q}")
        scale_tile(0, 0, 0)
        scale_tile(0, 0, 1)
        quantise_h3_tile(0, 0, 0)
        quantise_h3_tile(0, 0, 1)
        sweep_passes(0)
        turn(0, 3, (0, 1), "b4")
        scale(0, 1)
        clear(w4s[1][:, 0:2, :])
        load_upper(0)
        quantise_h3(0, 1)
        sweep_passes(1)
        turn(1, 0, (0, 1), "b5")
        turn(1, 1, (0, 1), "b6")
        scale(0, 2)
        clear(w4s[1][:, 2:4, :])
        load_upper(2)
        load_x0()
        quantise_h3(0, 2)
        sweep_passes(2)
        turn(1, 2, (0, 1), "b7")
        scale(0, 3)
        clear(w5s[:])
        quantise_h3(0, 3)
        turn(1, 3, (0, 1), "b4")
        for g in range(NG):
            multiply(1, g)
        join(1, 0)
        sweep_passes(3)
        for q in range(4):
            relu_move(0, q)
            if q > 0:
                join(1, q)
        load_late()
        for g in range(NG):
            quantise_h3(1, g)
        token_sweep(0, ("b5", "b6", "b0", "b1"))
        b5_rows = spread_rows(32, "b7")
        for i in range(2):
            for o in (2, 3):
                add_b4(0, i, o)
        for i in range(2):
            x_odd(0, i)
        nc.scalar.copy(out=b5bc[:], in_=b5_rows[:].rearrange("m n c -> m (n c)"))
        channel_tiles(1, 0, "b2")
        relu_move(1, 0)
        interleave_on_scalar(0, 0)
        interleave(0, 1)
        x_even(0, 0)
        quantise_moved(0, 1)
        quantise_moved(0, 0)
        channel_tiles(1, 1, "b3")
        turn_back(0, 0, (2, 3), "b7")
        turn_back(0, 1, (2, 3), "b4")
        relu_move(1, 1)
        relu_back(0, 0, (2, 3))
        x_even(0, 1)
        quantise_back(0, 0, (2, 3))
        channel_tiles(1, 2, "b5")
        relu_move(1, 2)
        channel_tiles(1, 3, "b6")
        relu_move(1, 3)
        relu_back(0, 1, (2, 3))
        stage2(0, 0, "b1")
        token_tile(1, 0, 2, "b0")
        token_tile(1, 0, 3, "b2")
        x_even(1, 0)
        x_even(1, 1)
        add_m(0, 0)
        store(0, 0, HALF)
        quantise_back(0, 1, (2, 3))
        stage2(0, 1, "b3")
        add_b4(1, 0, 2)
        add_b4(1, 0, 3)
        x_odd(1, 0)
        x_odd(1, 1)
        interleave_on_scalar(1, 0)
        interleave(1, 1)
        turn_back(1, 0, (2, 3), "b7")
        token_tile(1, 1, 2, "b4")
        token_tile(1, 1, 3, "b6")
        add_m(0, 1)
        relu_back(1, 0, (2, 3))
        store(0, 1, HALF)
        quantise_moved(1, 1)
        quantise_moved(1, 0)
        add_b4(1, 1, 2)
        quantise_back(1, 0, (2, 3))
        turn_back(1, 1, (2,), "b1")
        add_b4(1, 1, 3)
        stage2(1, 0, "b0")
        relu_back(1, 1, (2,))
        turn_back(1, 1, (3,), "b3")
        last = zero_banks(("b2", "b5"))
        add_m(1, 0)
        quantise_back(1, 1, (2,))
        relu_back(1, 1, (3,))
        quantise_back(1, 1, (3,))
        stage2_last(1, 1, last)
        store(1, 0, 256)
        finish_last(1, 1, last)
